import numpy as np
import ml_dtypes


def mxq(x, axis, fmt="e4m3"):
    dtype, down = {"e4m3": (ml_dtypes.float8_e4m3fn, 7), "e5m2": (ml_dtypes.float8_e5m2, 14)}[fmt]
    v = np.moveaxis(np.asarray(x, np.float32).astype(ml_dtypes.bfloat16).astype(np.float64), axis, -1)
    blocks = v.reshape(v.shape[:-1] + (-1, 32))
    amax = np.abs(blocks).max(-1, keepdims=True)
    byte = np.maximum(np.where(amax > 0, np.frexp(amax)[1] - 1 + 127, 0) - down, 1)
    scale = np.exp2(byte - 127.0)
    codes = (blocks / scale).astype(np.float32).astype(dtype).astype(np.float64)
    return np.moveaxis((codes * scale).reshape(v.shape), -1, axis)


WIDE = False


def mx_kscale(k):
    if not WIDE:
        return np.ones(k)
    levels = np.array([10, -10, 5, -5, 0])
    a = np.random.permutation(np.resize(levels, k // 512 * 4)).reshape(k // 512, 4)
    idx = np.arange(k)
    return np.exp2(a[idx // 512, idx % 128 // 32])


BF16 = ml_dtypes.bfloat16


def bf(x):
    return np.asarray(x, np.float32).astype(BF16)


def f64(x):
    return np.asarray(x).astype(np.float64)


B, R, N, D, L = 2, 4, 512, 512, 2
RN = R * N
P_EDGE = 0.02


def setup_inputs():
    s = mx_kscale(D)
    return {"x": bf(np.random.standard_normal((B, N, D)) * 0.6 * s),
            "adj": bf(np.random.random((B, R, N, N)) < P_EDGE),
            "wr": bf(np.random.standard_normal((R, D, D)) * 3.0 / np.sqrt(D) / s[:, None]),
            "br": bf(np.random.standard_normal((R, D)) * 0.3),
            "w0": bf(np.random.standard_normal((D, D)) * 3.0 / np.sqrt(D) / s[:, None]),
            "b0": bf(np.random.standard_normal(D) * 0.5)}


def reference(x, adj, wr, br, w0, b0):
    a = f64(adj)
    den = a.sum(axis=(1, 3))[:, :, None] + 1.0
    xq = mxq(f64(x), 2, "e4m3")
    msg = (xq[:, None] @ mxq(f64(wr), 1, "e4m3")[None]) + f64(br)[None, :, None, :]
    a_flat = a.transpose(0, 2, 1, 3).reshape(B, N, RN)
    agg = mxq(a_flat, 2, "e4m3") @ mxq(msg.reshape(B, RN, D), 1, "e4m3")
    self_term = (xq @ mxq(f64(w0), 0, "e4m3")) + f64(b0)
    return np.maximum((agg + self_term) / den, 0.0)

@@ -1,0 +1,270 @@
+from contextlib import ExitStack
+
+import concourse.mybir as mybir
+from concourse.masks import make_identity
+
+F32 = mybir.dt.float32
+BF16 = mybir.dt.bfloat16
+U32 = mybir.dt.uint32
+U8 = mybir.dt.uint8
+FP8X4 = mybir.dt.float8_e4m3fn_x4
+ADD = mybir.AluOpType.add
+COPY = mybir.ActivationFunctionType.Copy
+RELU = mybir.ActivationFunctionType.Relu
+
+P = 128
+B, R, N, D = 2, 4, 512, 512
+NT = N // P
+PACK = 4
+W0 = R
+FLOPS = 2 * B * (R + 1) * N * D * D + 2 * B * N * R * N * D
+
+NODES = "(u p e) f -> p u e f"
+TILES = "p (u e) f -> p u e f"
+
+
+def tile_rgcn_layer_pa_kernel(tc, x, adj, wr, br, w0, b0, out):
+    nc = tc.nc
+    with ExitStack() as ctx:
+        const = ctx.enter_context(tc.tile_pool(name="const", bufs=1))
+        inp = ctx.enter_context(tc.tile_pool(name="inp", bufs=1))
+        keep = ctx.enter_context(tc.tile_pool(name="keep", bufs=1))
+        grp = ctx.enter_context(tc.tile_pool(name="grp", bufs=3))
+        fin = ctx.enter_context(tc.tile_pool(name="fin", bufs=4))
+        ps_acc = ctx.enter_context(tc.psum_pool(name="ps_acc", bufs=4))
+        ps_ms = ctx.enter_context(tc.psum_pool(name="ps_ms", bufs=2))
+        ps_tp = ctx.enter_context(tc.psum_pool(name="ps_tp", bufs=2))
+
+        ident_f = const.tile([P, P], F32, name="ident_f")
+        ident_b = const.tile([P, P], BF16, name="ident_b")
+        brows = const.tile([P, D], BF16, name="brows")
+        bias_bc = const.tile([P, R + 1, D], BF16, name="bias_bc")
+        den_raw = const.tile([P, B * NT], F32, name="den_raw")
+        den_one = const.tile([P, B * NT], F32, name="den_one")
+        rden = const.tile([P, B * NT], F32, name="rden")
+        junk = const.tile([P, R * N], BF16, name="junk")
+
+        nc.vector.memset(brows, 0.0)
+        make_identity(nc, ident_b)
+        make_identity(nc, ident_f)
+
+        x_sb = [inp.tile([P, NT, D], BF16, name="x_sb%d" % b) for b in range(B)]
+        w_sb = [inp.tile([P, PACK, D], BF16, name="w_sb%d" % i) for i in range(R + 1)]
+        adj_sb = [inp.tile([P, R, NT, N], BF16, name="adj_sb%d" % b) for b in range(B)]
+
+        def load_x(b):
+            nc.sync.dma_start(out=x_sb[b].rearrange(TILES, u=2), in_=x[b].rearrange(NODES, u=2, e=2))
+
+        def load_w(i):
+            src = w0 if i == W0 else wr[i]
+            nc.sync.dma_start(out=w_sb[i].rearrange(TILES, u=2), in_=src.rearrange(NODES, u=2, e=2))
+
+        def load_adj(b, r):
+            nc.sync.dma_start(
+                out=adj_sb[b][:, r].rearrange(TILES, u=2), in_=adj[b, r].rearrange(NODES, u=2, e=2)
+            )
+
+        load_x(0)
+        nc.sync.dma_start(out=brows[0:R, :], in_=br)
+        nc.sync.dma_start(out=brows[R : R + 1, :], in_=b0.rearrange("(o d) -> o d", o=1))
+        load_w(0)
+        load_w(1)
+        load_adj(0, 0)
+        load_adj(0, 1)
+        load_w(2)
+        load_adj(0, 2)
+        load_adj(0, 3)
+        load_w(3)
+        load_w(W0)
+        load_x(1)
+        for r in range(R):
+            load_adj(1, r)
+
+        def packed(name):
+            words = keep.tile([P, 512], U32, name=name + "_c", align_bytes=64)
+            scales = keep.tile([P, 512], U8, name=name + "_s", align_bytes=64)
+            return words, scales
+
+        xq = [packed("xq%d" % b) for b in range(B)]
+        wq = [packed("wq%d" % i) for i in range(R + 1)]
+        aq = [packed("aq%d" % k) for k in range(B * R)]
+        mq = [packed("mq%d" % k) for k in range(B * R)]
+
+        def quantise(dst, grouped):
+            nc.vector.quantize_mx(out=dst[0].bitcast(FP8X4), scales=dst[1], in_=grouped)
+
+        def mx(acc, lhs, lcols, rhs, rcols, start, stop):
+            nc.tensor.matmul_mx(
+                out=acc,
+                lhsT=lhs[0][:, lcols].bitcast(FP8X4),
+                lhsT_scale=lhs[1][:, lcols],
+                rhs=rhs[0][:, rcols].bitcast(FP8X4),
+                rhs_scale=rhs[1][:, rcols],
+                start=start,
+                stop=stop,
+            )
+
+        def cols(i):
+            return slice(P * i, P * (i + 1))
+
+        def bias_row(i, evac):
+            bank = ps_tp.tile([P, D], F32, tag="tp", name="bias_ps")
+            nc.tensor.matmul(
+                out=bank, lhsT=ident_b[:, i : i + 1].to_broadcast([P, P]), rhs=brows, start=True, stop=True
+            )
+            evac(out=bias_bc[:, i, :], in_=bank)
+
+        def flip(rows, evac):
+            grouped = grp.tile([P, PACK * 512], BF16, tag="flipped", name="flipped", align_bytes=64)
+            words_out = grouped.bitcast(F32).rearrange("q (c v) -> q c v", v=2)
+            for h in range(2):
+                bank = ps_tp.tile([P, 2, 2 * P], F32, tag="tp", name="flip_ps")
+                for a in range(2):
+                    words_in = rows[:, 2 * h + a, :].bitcast(F32)
+                    for v in range(2):
+                        nc.tensor.transpose(bank[:, v, cols(a)], words_in[:, cols(v)], ident_f)
+                evac(out=words_out[:, 2 * P * h : 2 * P * (h + 1), :], in_=bank.rearrange("q v c -> q c v"))
+            return grouped
+
+        def regroup(i, copy):
+            grouped = grp.tile([P, PACK * D], BF16, tag="wg", name="wg", align_bytes=64)
+            copy(
+                out=grouped.rearrange("q (c i t) -> q c t i", i=4, t=PACK),
+                in_=w_sb[i].rearrange("q t (c i) -> q c t i", i=4),
+            )
+            return grouped
+
+        def messages(k, dc, grouped):
+            b, r = divmod(k, R)
+            bank = ps_ms.tile([P, NT, P], F32, tag="ms", name="ms_ps")
+            for t in range(NT):
+                mx(bank[:, t, :], xq[b], cols(t), wq[r], cols(dc), True, True)
+            nc.vector.tensor_tensor(
+                out=grouped.rearrange("p (d t) -> p d t", t=PACK)[:, cols(dc), :],
+                in0=bank.rearrange("p t d -> p d t"),
+                in1=bias_bc[:, r, cols(dc)].unsqueeze(2).to_broadcast([P, P, PACK]),
+                op=ADD,
+            )
+
+        acc = {}
+
+        def self_term(b, m, start):
+            if start:
+                acc[(b, m)] = ps_acc.tile([P, D], F32, tag="acc", name="acc_ps")
+            mx(acc[(b, m)], xq[b], cols(m), wq[W0], slice(0, D), start, False)
+
+        def aggregate(k, m, start, stop):
+            b = k // R
+            if start:
+                acc[(b, m)] = ps_acc.tile([P, D], F32, tag="acc", name="acc_ps")
+            mx(acc[(b, m)], aq[k], cols(m), mq[k], slice(0, D), start, stop)
+
+        def den_tensor(b, m):
+            bank = ps_tp.tile([P, P], F32, tag="tp", name="den_ps")
+            for r in range(R):
+                for g in range(NT):
+                    nc.tensor.matmul(
+                        out=bank,
+                        lhsT=ident_b,
+                        rhs=adj_sb[b][:, r, m, cols(g)],
+                        start=(r == 0 and g == 0),
+                        stop=(r == R - 1 and g == NT - 1),
+                    )
+            c = NT * b + m
+            nc.scalar.activation(out=junk[:, 0:P], in_=bank, func=COPY, accum_out=den_raw[:, c : c + 1])
+
+        def den_scalar(b, m):
+            c = NT * b + m
+            nc.scalar.activation(
+                out=junk.rearrange("p (r j) -> p r j", r=R),
+                in_=adj_sb[b][:, :, m, :],
+                func=COPY,
+                accum_out=den_raw[:, c : c + 1],
+            )
+
+        def den_close(b):
+            these = slice(NT * b, NT * (b + 1))
+            nc.vector.tensor_scalar_add(out=den_one[:, these], in0=den_raw[:, these], scalar1=1.0)
+            nc.vector.reciprocal(out=rden[:, these], in_=den_one[:, these])
+
+        sums = {}
+
+        def add_b0(b, m):
+            sums[(b, m)] = fin.tile([P, D], F32, tag="fsum", name="fsum")
+            nc.vector.tensor_tensor(out=sums[(b, m)], in0=acc[(b, m)], in1=bias_bc[:, W0, :], op=ADD)
+
+        def finish(b, m):
+            res = fin.tile([P, D], F32, tag="res", name="res")
+            c = NT * b + m
+            nc.scalar.activation(out=res, in_=sums[(b, m)], func=RELU, scale=rden[:, c : c + 1])
+            u, e = divmod(m, 2)
+            nc.sync.dma_start(out=out[b].rearrange(NODES, u=2, e=2)[:, u, e, :], in_=res)
+
+        vcopy = nc.vector.tensor_copy
+        scopy = nc.scalar.copy
+
+        bias_row(0, vcopy)
+        xg = flip(x_sb[0], scopy)
+        wg = regroup(0, vcopy)
+        quantise(xq[0], xg)
+        quantise(wq[0], wg)
+        wg_next = regroup(1, scopy)
+        bias_row(1, scopy)
+        ag = {0: flip(adj_sb[0][:, 0], scopy)}
+
+        for k in range(B * R):
+            b, r = divmod(k, R)
+            mg = grp.tile([P, PACK * D], BF16, tag="mg", name="mg", align_bytes=64)
+            messages(k, 0, mg)
+            messages(k, 1, mg)
+            if b == 0 and r + 1 < R:
+                quantise(wq[r + 1], wg_next)
+            if k == 3:
+                quantise(wq[W0], wg_next)
+            for m in range(NT):
+                if k == 5:
+                    self_term(1, m, True)
+                if k >= 1:
+                    prev = k - 1
+                    aggregate(prev, m, prev == 0, prev == R - 1)
+                if k == 4:
+                    add_b0(0, m)
+                if m == 1:
+                    messages(k, 2, mg)
+                if m == 2:
+                    messages(k, 3, mg)
+            if k == 3:
+                for m in range(NT):
+                    self_term(0, m, False)
+            quantise(aq[k], ag[k])
+            quantise(mq[k], mg)
+            if k + 1 < B * R:
+                ag[k + 1] = flip(adj_sb[(k + 1) // R][:, (k + 1) % R], scopy)
+            if k == 0:
+                wg_next = regroup(2, scopy)
+                bias_row(2, scopy)
+            if k == 1:
+                wg_next = regroup(3, scopy)
+                bias_row(3, scopy)
+                den_tensor(0, 0)
+            if k == 2:
+                wg_next = regroup(W0, scopy)
+                bias_row(W0, scopy)
+                den_tensor(0, 1)
+                den_tensor(0, 2)
+                xg = flip(x_sb[1], scopy)
+            if k == 3:
+                quantise(xq[1], xg)
+                den_tensor(0, 3)
+                den_close(0)
+            if k == 4:
+                den_tensor(1, 0)
+            if k > 4:
+                den_scalar(1, k - 4)
+            if k >= 4:
+                finish(0, k - 4)
+        den_close(1)
+        for m in range(NT):
+            aggregate(B * R - 1, m, False, True)
+            add_b0(1, m)
+            finish(1, m)

@@ -9,6 +9,7 @@ U32 = mybir.dt.uint32
 U8 = mybir.dt.uint8
 FP8X4 = mybir.dt.float8_e4m3fn_x4
 ADD = mybir.AluOpType.add
+MULT = mybir.AluOpType.mult
 COPY = mybir.ActivationFunctionType.Copy
 RELU = mybir.ActivationFunctionType.Relu
 
@@ -17,10 +18,15 @@ B, R, N, D = 2, 4, 512, 512
 NT = N // P
 PACK = 4
 W0 = R
+LAST = B * R - 1
 FLOPS = 2 * B * (R + 1) * N * D * D + 2 * B * N * R * N * D
 
 NODES = "(u p e) f -> p u e f"
 TILES = "p (u e) f -> p u e f"
+
+DEN_T = 2
+DEN_ROUND = ((), (0,), (1,), (2,), (3,), (4, 5), (6,), (7,))
+G_SHARE = 80
 
 
 def tile_rgcn_layer_pa_kernel(tc, x, adj, wr, br, w0, b0, out):
@@ -30,7 +36,8 @@ def tile_rgcn_layer_pa_kernel(tc, x, adj, wr, br, w0, b0, out):
         inp = ctx.enter_context(tc.tile_pool(name="inp", bufs=1))
         keep = ctx.enter_context(tc.tile_pool(name="keep", bufs=1))
         grp = ctx.enter_context(tc.tile_pool(name="grp", bufs=3))
-        fin = ctx.enter_context(tc.tile_pool(name="fin", bufs=4))
+        ring = ctx.enter_context(tc.tile_pool(name="ring", bufs=1))
+        fin = ctx.enter_context(tc.tile_pool(name="fin", bufs=8))
         ps_acc = ctx.enter_context(tc.psum_pool(name="ps_acc", bufs=4))
         ps_ms = ctx.enter_context(tc.psum_pool(name="ps_ms", bufs=2))
         ps_tp = ctx.enter_context(tc.psum_pool(name="ps_tp", bufs=2))
@@ -39,14 +46,11 @@ def tile_rgcn_layer_pa_kernel(tc, x, adj, wr, br, w0, b0, out):
         ident_b = const.tile([P, P], BF16, name="ident_b")
         brows = const.tile([P, D], BF16, name="brows")
         bias_bc = const.tile([P, R + 1, D], BF16, name="bias_bc")
-        den_raw = const.tile([P, B * NT], F32, name="den_raw")
+        den_t = const.tile([P, B * NT], F32, name="den_t")
+        den_s = const.tile([P, B * NT], F32, name="den_s")
         den_one = const.tile([P, B * NT], F32, name="den_one")
         rden = const.tile([P, B * NT], F32, name="rden")
         junk = const.tile([P, R * N], BF16, name="junk")
-
-        nc.vector.memset(brows, 0.0)
-        make_identity(nc, ident_b)
-        make_identity(nc, ident_f)
 
         x_sb = [inp.tile([P, NT, D], BF16, name="x_sb%d" % b) for b in range(B)]
         w_sb = [inp.tile([P, PACK, D], BF16, name="w_sb%d" % i) for i in range(R + 1)]
@@ -64,22 +68,6 @@ def tile_rgcn_layer_pa_kernel(tc, x, adj, wr, br, w0, b0, out):
                 out=adj_sb[b][:, r].rearrange(TILES, u=2), in_=adj[b, r].rearrange(NODES, u=2, e=2)
             )
 
-        load_x(0)
-        nc.sync.dma_start(out=brows[0:R, :], in_=br)
-        nc.sync.dma_start(out=brows[R : R + 1, :], in_=b0.rearrange("(o d) -> o d", o=1))
-        load_w(0)
-        load_w(1)
-        load_adj(0, 0)
-        load_adj(0, 1)
-        load_w(2)
-        load_adj(0, 2)
-        load_adj(0, 3)
-        load_w(3)
-        load_w(W0)
-        load_x(1)
-        for r in range(R):
-            load_adj(1, r)
-
         def packed(name):
             words = keep.tile([P, 512], U32, name=name + "_c", align_bytes=64)
             scales = keep.tile([P, 512], U8, name=name + "_s", align_bytes=64)
@@ -90,8 +78,8 @@ def tile_rgcn_layer_pa_kernel(tc, x, adj, wr, br, w0, b0, out):
         aq = [packed("aq%d" % k) for k in range(B * R)]
         mq = [packed("mq%d" % k) for k in range(B * R)]
 
-        def quantise(dst, grouped):
-            nc.vector.quantize_mx(out=dst[0].bitcast(FP8X4), scales=dst[1], in_=grouped)
+        def quantise(dst, src):
+            nc.vector.quantize_mx(out=dst[0].bitcast(FP8X4), scales=dst[1], in_=src)
 
         def mx(acc, lhs, lcols, rhs, rcols, start, stop):
             nc.tensor.matmul_mx(
@@ -107,42 +95,76 @@ def tile_rgcn_layer_pa_kernel(tc, x, adj, wr, br, w0, b0, out):
         def cols(i):
             return slice(P * i, P * (i + 1))
 
-        def bias_row(i, evac):
-            bank = ps_tp.tile([P, D], F32, tag="tp", name="bias_ps")
+        vcopy = nc.vector.tensor_copy
+        scopy = nc.scalar.copy
+
+        def gcopy(out, in_):
+            nc.gpsimd.tensor_scalar(out=out, in0=in_, scalar1=1.0, scalar2=0.0, op0=MULT, op1=ADD)
+
+        banks = {}
+        grouped = {}
+
+        def quantise_part(dst, src, h):
+            nc.vector.quantize_mx(
+                out=dst[0][:, 256 * h : 256 * (h + 1)].bitcast(FP8X4),
+                scales=dst[1][:, 256 * h : 256 * (h + 1)],
+                in_=src[:, 1024 * h : 1024 * (h + 1)],
+            )
+
+        def bias_mm(i):
+            banks[("bias", i)] = ps_tp.tile([P, D], F32, tag="tp", name="bias_ps")
             nc.tensor.matmul(
-                out=bank, lhsT=ident_b[:, i : i + 1].to_broadcast([P, P]), rhs=brows, start=True, stop=True
+                out=banks[("bias", i)],
+                lhsT=ident_b[:, i : i + 1].to_broadcast([P, P]),
+                rhs=brows,
+                start=True,
+                stop=True,
             )
-            evac(out=bias_bc[:, i, :], in_=bank)
 
-        def flip(rows, evac):
-            grouped = grp.tile([P, PACK * 512], BF16, tag="flipped", name="flipped", align_bytes=64)
-            words_out = grouped.bitcast(F32).rearrange("q (c v) -> q c v", v=2)
-            for h in range(2):
-                bank = ps_tp.tile([P, 2, 2 * P], F32, tag="tp", name="flip_ps")
-                for a in range(2):
-                    words_in = rows[:, 2 * h + a, :].bitcast(F32)
-                    for v in range(2):
-                        nc.tensor.transpose(bank[:, v, cols(a)], words_in[:, cols(v)], ident_f)
-                evac(out=words_out[:, 2 * P * h : 2 * P * (h + 1), :], in_=bank.rearrange("q v c -> q c v"))
-            return grouped
+        def bias_out(i, evac):
+            evac(out=bias_bc[:, i, :], in_=banks[("bias", i)])
 
-        def regroup(i, copy):
-            grouped = grp.tile([P, PACK * D], BF16, tag="wg", name="wg", align_bytes=64)
+        def flip_mm(key, rows, h):
+            if h == 0:
+                grouped[key] = grp.tile([P, PACK * 512], BF16, tag="flipped", name="flipped", align_bytes=64)
+            bank = ps_tp.tile([P, 2, 2 * P], F32, tag="tp", name="flip_ps")
+            banks[(key, h)] = bank
+            for a in range(2):
+                words_in = rows[:, 2 * h + a, :].bitcast(F32)
+                for v in range(2):
+                    nc.tensor.transpose(bank[:, v, cols(a)], words_in[:, cols(v)], ident_f)
+
+        def flip_out(key, h, evac):
+            words_out = grouped[key].bitcast(F32).rearrange("q (c v) -> q c v", v=2)
+            evac(
+                out=words_out[:, 2 * P * h : 2 * P * (h + 1), :],
+                in_=banks[(key, h)].rearrange("q v c -> q c v"),
+            )
+
+        def adj_rows(k):
+            return adj_sb[k // R][:, k % R]
+
+        def ring_tile(slot):
+            return ring.tile([P, PACK * D], BF16, tag="ring%d" % (slot % 3), name="ring", align_bytes=64)
+
+        def regroup(i, copy, lo, hi):
             copy(
-                out=grouped.rearrange("q (c i t) -> q c t i", i=4, t=PACK),
-                in_=w_sb[i].rearrange("q t (c i) -> q c t i", i=4),
+                out=grouped[("w", i)].rearrange("q (c i t) -> q c t i", i=4, t=PACK)[:, lo:hi],
+                in_=w_sb[i].rearrange("q t (c i) -> q c t i", i=4)[:, lo:hi],
             )
-            return grouped
 
-        def messages(k, dc, grouped):
+        def fill(k, dc):
             b, r = divmod(k, R)
             bank = ps_ms.tile([P, NT, P], F32, tag="ms", name="ms_ps")
+            banks[("ms", k, dc)] = bank
             for t in range(NT):
                 mx(bank[:, t, :], xq[b], cols(t), wq[r], cols(dc), True, True)
+
+        def bias_add(k, dc):
             nc.vector.tensor_tensor(
-                out=grouped.rearrange("p (d t) -> p d t", t=PACK)[:, cols(dc), :],
-                in0=bank.rearrange("p t d -> p d t"),
-                in1=bias_bc[:, r, cols(dc)].unsqueeze(2).to_broadcast([P, P, PACK]),
+                out=grouped[("m", k)].rearrange("p (d t) -> p d t", t=PACK)[:, cols(dc), :],
+                in0=banks[("ms", k, dc)].rearrange("p t d -> p d t"),
+                in1=bias_bc[:, k % R, cols(dc)].unsqueeze(2).to_broadcast([P, P, PACK]),
                 op=ADD,
             )
 
@@ -153,38 +175,43 @@ def tile_rgcn_layer_pa_kernel(tc, x, adj, wr, br, w0, b0, out):
                 acc[(b, m)] = ps_acc.tile([P, D], F32, tag="acc", name="acc_ps")
             mx(acc[(b, m)], xq[b], cols(m), wq[W0], slice(0, D), start, False)
 
-        def aggregate(k, m, start, stop):
+        def aggregate(k, m):
             b = k // R
-            if start:
+            if k == 0:
                 acc[(b, m)] = ps_acc.tile([P, D], F32, tag="acc", name="acc_ps")
-            mx(acc[(b, m)], aq[k], cols(m), mq[k], slice(0, D), start, stop)
+            mx(acc[(b, m)], aq[k], cols(m), mq[k], slice(0, D), k == 0, k % R == R - 1)
 
-        def den_tensor(b, m):
+        def den_mm(j):
+            b, m = divmod(j, NT)
             bank = ps_tp.tile([P, P], F32, tag="tp", name="den_ps")
-            for r in range(R):
+            banks[("den", j)] = bank
+            for r in range(DEN_T):
                 for g in range(NT):
                     nc.tensor.matmul(
                         out=bank,
                         lhsT=ident_b,
                         rhs=adj_sb[b][:, r, m, cols(g)],
                         start=(r == 0 and g == 0),
-                        stop=(r == R - 1 and g == NT - 1),
+                        stop=(r == DEN_T - 1 and g == NT - 1),
                     )
-            c = NT * b + m
-            nc.scalar.activation(out=junk[:, 0:P], in_=bank, func=COPY, accum_out=den_raw[:, c : c + 1])
 
-        def den_scalar(b, m):
-            c = NT * b + m
+        def den_out(j):
+            nc.scalar.activation(out=junk[:, 0:P], in_=banks[("den", j)], func=COPY, accum_out=den_t[:, j : j + 1])
+
+        def den_scalar(j):
+            b, m = divmod(j, NT)
             nc.scalar.activation(
-                out=junk.rearrange("p (r j) -> p r j", r=R),
-                in_=adj_sb[b][:, :, m, :],
+                out=junk.rearrange("p (r j) -> p r j", r=R)[:, DEN_T:R],
+                in_=adj_sb[b][:, DEN_T:R, m, :],
                 func=COPY,
-                accum_out=den_raw[:, c : c + 1],
+                accum_out=den_s[:, j : j + 1],
             )
 
         def den_close(b):
             these = slice(NT * b, NT * (b + 1))
-            nc.vector.tensor_scalar_add(out=den_one[:, these], in0=den_raw[:, these], scalar1=1.0)
+            nc.vector.scalar_tensor_tensor(
+                out=den_one[:, these], in0=den_t[:, these], scalar=1.0, in1=den_s[:, these], op0=ADD, op1=ADD
+            )
             nc.vector.reciprocal(out=rden[:, these], in_=den_one[:, these])
 
         sums = {}
@@ -200,71 +227,106 @@ def tile_rgcn_layer_pa_kernel(tc, x, adj, wr, br, w0, b0, out):
             u, e = divmod(m, 2)
             nc.sync.dma_start(out=out[b].rearrange(NODES, u=2, e=2)[:, u, e, :], in_=res)
 
-        vcopy = nc.vector.tensor_copy
-        scopy = nc.scalar.copy
+        with tc.manual_schedule():
+            nc.vector.memset(brows, 0.0)
+            make_identity(nc, ident_f)
+            make_identity(nc, ident_b)
+            for u in range(2):
+                nc.sync.dma_start(
+                    out=x_sb[0].rearrange(TILES, u=2)[:, u], in_=x[0].rearrange(NODES, u=2, e=2)[:, u]
+                )
+            nc.sync.dma_start(out=brows[0:R, :], in_=br)
+            nc.sync.dma_start(out=brows[R : R + 1, :], in_=b0.rearrange("(o d) -> o d", o=1))
+            load_w(0)
+            load_w(1)
+            load_adj(0, 0)
+            load_w(2)
+            load_adj(0, 1)
+            load_adj(0, 2)
+            load_adj(0, 3)
+            load_w(3)
+            load_w(W0)
+            load_x(1)
+            for r in range(R):
+                load_adj(1, r)
 
-        bias_row(0, vcopy)
-        xg = flip(x_sb[0], scopy)
-        wg = regroup(0, vcopy)
-        quantise(xq[0], xg)
-        quantise(wq[0], wg)
-        wg_next = regroup(1, scopy)
-        bias_row(1, scopy)
-        ag = {0: flip(adj_sb[0][:, 0], scopy)}
+            grouped[("w", 0)] = ring_tile(2)
+            for h in range(2):
+                flip_mm("x0", x_sb[0], h)
+                flip_out("x0", h, scopy)
+            quantise_part(xq[0], grouped["x0"], 0)
+            regroup(0, vcopy, 0, 64)
+            regroup(0, scopy, 64, 128)
+            quantise_part(xq[0], grouped["x0"], 1)
+            quantise_part(wq[0], grouped[("w", 0)], 0)
+            bias_mm(0)
+            bias_out(0, scopy)
+            fill(0, 0)
+            fill(0, 1)
+            quantise_part(wq[0], grouped[("w", 0)], 1)
+            for h in range(2):
+                flip_mm(("a", 0), adj_rows(0), h)
 
-        for k in range(B * R):
-            b, r = divmod(k, R)
-            mg = grp.tile([P, PACK * D], BF16, tag="mg", name="mg", align_bytes=64)
-            messages(k, 0, mg)
-            messages(k, 1, mg)
-            if b == 0 and r + 1 < R:
-                quantise(wq[r + 1], wg_next)
-            if k == 3:
-                quantise(wq[W0], wg_next)
-            for m in range(NT):
-                if k == 5:
-                    self_term(1, m, True)
+            for k in range(B * R):
+                grouped[("m", k)] = ring_tile(k)
+                if k < R:
+                    grouped[("w", k + 1)] = ring_tile(k + 2)
+                    regroup(k + 1, gcopy, 0, G_SHARE)
+                for h in range(2):
+                    flip_out(("a", k), h, scopy)
+                if k < R:
+                    regroup(k + 1, scopy, G_SHARE, 128)
+                for j in DEN_ROUND[k]:
+                    den_scalar(j)
+                bias_add(k, 0)
+                bias_add(k, 1)
+                fill(k, 2)
+                bias_add(k, 2)
                 if k >= 1:
-                    prev = k - 1
-                    aggregate(prev, m, prev == 0, prev == R - 1)
-                if k == 4:
-                    add_b0(0, m)
-                if m == 1:
-                    messages(k, 2, mg)
-                if m == 2:
-                    messages(k, 3, mg)
-            if k == 3:
-                for m in range(NT):
-                    self_term(0, m, False)
-            quantise(aq[k], ag[k])
-            quantise(mq[k], mg)
-            if k + 1 < B * R:
-                ag[k + 1] = flip(adj_sb[(k + 1) // R][:, (k + 1) % R], scopy)
-            if k == 0:
-                wg_next = regroup(2, scopy)
-                bias_row(2, scopy)
-            if k == 1:
-                wg_next = regroup(3, scopy)
-                bias_row(3, scopy)
-                den_tensor(0, 0)
-            if k == 2:
-                wg_next = regroup(W0, scopy)
-                bias_row(W0, scopy)
-                den_tensor(0, 1)
-                den_tensor(0, 2)
-                xg = flip(x_sb[1], scopy)
-            if k == 3:
-                quantise(xq[1], xg)
-                den_tensor(0, 3)
-                den_close(0)
-            if k == 4:
-                den_tensor(1, 0)
-            if k > 4:
-                den_scalar(1, k - 4)
-            if k >= 4:
-                finish(0, k - 4)
-        den_close(1)
-        for m in range(NT):
-            aggregate(B * R - 1, m, False, True)
-            add_b0(1, m)
-            finish(1, m)
+                    aggregate(k - 1, 0)
+                fill(k, 3)
+                bias_add(k, 3)
+                if k == R:
+                    add_b0(0, 0)
+                for m in range(1, NT):
+                    if k >= 1:
+                        aggregate(k - 1, m)
+                    if k == R:
+                        add_b0(0, m)
+                if k < R:
+                    bias_mm(k + 1)
+                    bias_out(k + 1, scopy)
+                for j in DEN_ROUND[k]:
+                    den_mm(j)
+                    den_out(j)
+                if k == 2:
+                    for h in range(2):
+                        flip_mm("x1", x_sb[1], h)
+                        flip_out("x1", h, scopy)
+                if k == R - 1:
+                    quantise(xq[1], grouped["x1"])
+                if k < R:
+                    quantise(wq[k + 1], grouped[("w", k + 1)])
+                quantise(aq[k], grouped[("a", k)])
+                quantise(mq[k], grouped[("m", k)])
+                if k == R + 1:
+                    den_close(0)
+                if k >= R + 1:
+                    finish(0, k - R - 1)
+                if k < LAST:
+                    fill(k + 1, 0)
+                    fill(k + 1, 1)
+                    if k == R - 1:
+                        for m in range(NT):
+                            self_term(0, m, False)
+                    for h in range(2):
+                        flip_mm(("a", k + 1), adj_rows(k + 1), h)
+                    if k == R:
+                        for m in range(NT):
+                            self_term(1, m, True)
+            den_close(1)
+            finish(0, 3)
+            for m in range(NT):
+                aggregate(LAST, m)
+                add_b0(1, m)
+                finish(1, m)

@@ -25,7 +25,7 @@ NODES = "(u p e) f -> p u e f"
 TILES = "p (u e) f -> p u e f"
 
 DEN_T = 2
-DEN_ROUND = ((), (0,), (1,), (2,), (3,), (4, 5), (6,), (7,))
+DEN_ROUND = ((), (0,), (1,), (2,), (3,), (4,), (5,), (6, 7))
 G_SHARE = 80
 
 
@@ -39,8 +39,7 @@ def tile_rgcn_layer_pa_kernel(tc, x, adj, wr, br, w0, b0, out):
         ring = ctx.enter_context(tc.tile_pool(name="ring", bufs=1))
         fin = ctx.enter_context(tc.tile_pool(name="fin", bufs=8))
         ps_acc = ctx.enter_context(tc.psum_pool(name="ps_acc", bufs=4))
-        ps_ms = ctx.enter_context(tc.psum_pool(name="ps_ms", bufs=2))
-        ps_tp = ctx.enter_context(tc.psum_pool(name="ps_tp", bufs=2))
+        ps_work = ctx.enter_context(tc.psum_pool(name="ps_work", bufs=4))
 
         ident_f = const.tile([P, P], F32, name="ident_f")
         ident_b = const.tile([P, P], BF16, name="ident_b")
@@ -112,7 +111,7 @@ def tile_rgcn_layer_pa_kernel(tc, x, adj, wr, br, w0, b0, out):
             )
 
         def bias_mm(i):
-            banks[("bias", i)] = ps_tp.tile([P, D], F32, tag="tp", name="bias_ps")
+            banks[("bias", i)] = ps_work.tile([P, D], F32, tag="work", name="bias_ps")
             nc.tensor.matmul(
                 out=banks[("bias", i)],
                 lhsT=ident_b[:, i : i + 1].to_broadcast([P, P]),
@@ -127,7 +126,7 @@ def tile_rgcn_layer_pa_kernel(tc, x, adj, wr, br, w0, b0, out):
         def flip_mm(key, rows, h):
             if h == 0:
                 grouped[key] = grp.tile([P, PACK * 512], BF16, tag="flipped", name="flipped", align_bytes=64)
-            bank = ps_tp.tile([P, 2, 2 * P], F32, tag="tp", name="flip_ps")
+            bank = ps_work.tile([P, 2, 2 * P], F32, tag="work", name="flip_ps")
             banks[(key, h)] = bank
             for a in range(2):
                 words_in = rows[:, 2 * h + a, :].bitcast(F32)
@@ -155,7 +154,7 @@ def tile_rgcn_layer_pa_kernel(tc, x, adj, wr, br, w0, b0, out):
 
         def fill(k, dc):
             b, r = divmod(k, R)
-            bank = ps_ms.tile([P, NT, P], F32, tag="ms", name="ms_ps")
+            bank = ps_work.tile([P, NT, P], F32, tag="work", name="ms_ps")
             banks[("ms", k, dc)] = bank
             for t in range(NT):
                 mx(bank[:, t, :], xq[b], cols(t), wq[r], cols(dc), True, True)
@@ -183,7 +182,7 @@ def tile_rgcn_layer_pa_kernel(tc, x, adj, wr, br, w0, b0, out):
 
         def den_mm(j):
             b, m = divmod(j, NT)
-            bank = ps_tp.tile([P, P], F32, tag="tp", name="den_ps")
+            bank = ps_work.tile([P, P], F32, tag="work", name="den_ps")
             banks[("den", j)] = bank
             for r in range(DEN_T):
                 for g in range(NT):
@@ -240,13 +239,13 @@ def tile_rgcn_layer_pa_kernel(tc, x, adj, wr, br, w0, b0, out):
             load_w(0)
             load_w(1)
             load_adj(0, 0)
-            load_w(2)
             load_adj(0, 1)
+            load_x(1)
+            load_w(2)
             load_adj(0, 2)
             load_adj(0, 3)
             load_w(3)
             load_w(W0)
-            load_x(1)
             for r in range(R):
                 load_adj(1, r)
 
@@ -264,31 +263,20 @@ def tile_rgcn_layer_pa_kernel(tc, x, adj, wr, br, w0, b0, out):
             fill(0, 0)
             fill(0, 1)
             quantise_part(wq[0], grouped[("w", 0)], 1)
-            for h in range(2):
-                flip_mm(("a", 0), adj_rows(0), h)
+            fill(0, 2)
+            fill(0, 3)
 
             for k in range(B * R):
                 grouped[("m", k)] = ring_tile(k)
                 if k < R:
                     grouped[("w", k + 1)] = ring_tile(k + 2)
                     regroup(k + 1, gcopy, 0, G_SHARE)
-                for h in range(2):
-                    flip_out(("a", k), h, scopy)
-                if k < R:
                     regroup(k + 1, scopy, G_SHARE, 128)
                 for j in DEN_ROUND[k]:
                     den_scalar(j)
-                bias_add(k, 0)
-                bias_add(k, 1)
-                fill(k, 2)
-                bias_add(k, 2)
-                if k >= 1:
-                    aggregate(k - 1, 0)
-                fill(k, 3)
-                bias_add(k, 3)
-                if k == R:
-                    add_b0(0, 0)
-                for m in range(1, NT):
+                for dc in range(NT):
+                    bias_add(k, dc)
+                for m in range(NT):
                     if k >= 1:
                         aggregate(k - 1, m)
                     if k == R:
@@ -296,34 +284,40 @@ def tile_rgcn_layer_pa_kernel(tc, x, adj, wr, br, w0, b0, out):
                 if k < R:
                     bias_mm(k + 1)
                     bias_out(k + 1, scopy)
-                for j in DEN_ROUND[k]:
-                    den_mm(j)
-                    den_out(j)
-                if k == 2:
+                if k == 0:
+                    for h in range(2):
+                        flip_mm(("a", 0), adj_rows(0), h)
+                        flip_out(("a", 0), h, scopy)
+                if k < LAST:
+                    for h in range(2):
+                        flip_mm(("a", k + 1), adj_rows(k + 1), h)
+                        flip_out(("a", k + 1), h, scopy)
+                if k == 0:
                     for h in range(2):
                         flip_mm("x1", x_sb[1], h)
                         flip_out("x1", h, scopy)
-                if k == R - 1:
-                    quantise(xq[1], grouped["x1"])
+                for j in DEN_ROUND[k]:
+                    den_mm(j)
+                    den_out(j)
                 if k < R:
                     quantise(wq[k + 1], grouped[("w", k + 1)])
                 quantise(aq[k], grouped[("a", k)])
+                if k == 1:
+                    quantise(xq[1], grouped["x1"])
                 quantise(mq[k], grouped[("m", k)])
                 if k == R + 1:
                     den_close(0)
                 if k >= R + 1:
                     finish(0, k - R - 1)
                 if k < LAST:
-                    fill(k + 1, 0)
-                    fill(k + 1, 1)
-                    if k == R - 1:
-                        for m in range(NT):
-                            self_term(0, m, False)
-                    for h in range(2):
-                        flip_mm(("a", k + 1), adj_rows(k + 1), h)
-                    if k == R:
-                        for m in range(NT):
-                            self_term(1, m, True)
+                    for dc in range(NT):
+                        fill(k + 1, dc)
+                if k == R - 1:
+                    for m in range(NT):
+                        self_term(0, m, False)
+                if k == R:
+                    for m in range(NT):
+                        self_term(1, m, True)
             den_close(1)
             finish(0, 3)
             for m in range(NT):

@@ -24,8 +24,8 @@ FLOPS = 2 * B * (R + 1) * N * D * D + 2 * B * N * R * N * D
 NODES = "(u p e) f -> p u e f"
 TILES = "p (u e) f -> p u e f"
 
-DEN_T = 2
-DEN_ROUND = ((), (0,), (1,), (2,), (3,), (4,), (5,), (6, 7))
+DEN_T = (2, 0)
+DEN_ROUND = ((), (0,), (1,), (2,), (3, 4), (5,), (6,), (7,))
 G_SHARE = 80
 
 
@@ -123,10 +123,13 @@ def tile_rgcn_layer_pa_kernel(tc, x, adj, wr, br, w0, b0, out):
         def bias_out(i, evac):
             evac(out=bias_bc[:, i, :], in_=banks[("bias", i)])
 
-        def flip_mm(key, rows, h):
+        def flip_mm(key, rows, h, early=False):
             if h == 0:
                 grouped[key] = grp.tile([P, PACK * 512], BF16, tag="flipped", name="flipped", align_bytes=64)
-            bank = ps_work.tile([P, 2, 2 * P], F32, tag="work", name="flip_ps")
+            if early:
+                bank = ps_acc.tile([P, 2, 2 * P], F32, tag="acc", name="flip_ps")
+            else:
+                bank = ps_work.tile([P, 2, 2 * P], F32, tag="work", name="flip_ps")
             banks[(key, h)] = bank
             for a in range(2):
                 words_in = rows[:, 2 * h + a, :].bitcast(F32)
@@ -172,42 +175,50 @@ def tile_rgcn_layer_pa_kernel(tc, x, adj, wr, br, w0, b0, out):
         def self_term(b, m, start):
             if start:
                 acc[(b, m)] = ps_acc.tile([P, D], F32, tag="acc", name="acc_ps")
-            mx(acc[(b, m)], xq[b], cols(m), wq[W0], slice(0, D), start, False)
+            mx(acc[(b, m)], xq[b], cols(m), wq[W0], slice(0, D), start, not start)
 
         def aggregate(k, m):
             b = k // R
             if k == 0:
                 acc[(b, m)] = ps_acc.tile([P, D], F32, tag="acc", name="acc_ps")
-            mx(acc[(b, m)], aq[k], cols(m), mq[k], slice(0, D), k == 0, k % R == R - 1)
+            mx(acc[(b, m)], aq[k], cols(m), mq[k], slice(0, D), k == 0, k == LAST)
 
         def den_mm(j):
             b, m = divmod(j, NT)
+            if DEN_T[b] == 0:
+                return
             bank = ps_work.tile([P, P], F32, tag="work", name="den_ps")
             banks[("den", j)] = bank
-            for r in range(DEN_T):
+            for r in range(DEN_T[b]):
                 for g in range(NT):
                     nc.tensor.matmul(
                         out=bank,
                         lhsT=ident_b,
                         rhs=adj_sb[b][:, r, m, cols(g)],
                         start=(r == 0 and g == 0),
-                        stop=(r == DEN_T - 1 and g == NT - 1),
+                        stop=(r == DEN_T[b] - 1 and g == NT - 1),
                     )
 
         def den_out(j):
+            if DEN_T[j // NT] == 0:
+                return
             nc.scalar.activation(out=junk[:, 0:P], in_=banks[("den", j)], func=COPY, accum_out=den_t[:, j : j + 1])
 
         def den_scalar(j):
             b, m = divmod(j, NT)
             nc.scalar.activation(
-                out=junk.rearrange("p (r j) -> p r j", r=R)[:, DEN_T:R],
-                in_=adj_sb[b][:, DEN_T:R, m, :],
+                out=junk.rearrange("p (r j) -> p r j", r=R)[:, DEN_T[b] : R],
+                in_=adj_sb[b][:, DEN_T[b] : R, m, :],
                 func=COPY,
                 accum_out=den_s[:, j : j + 1],
             )
 
         def den_close(b):
             these = slice(NT * b, NT * (b + 1))
+            if DEN_T[b] == 0:
+                nc.vector.tensor_scalar_add(out=den_one[:, these], in0=den_s[:, these], scalar1=1.0)
+                nc.vector.reciprocal(out=rden[:, these], in_=den_one[:, these])
+                return
             nc.vector.scalar_tensor_tensor(
                 out=den_one[:, these], in0=den_t[:, these], scalar=1.0, in1=den_s[:, these], op0=ADD, op1=ADD
             )
@@ -280,21 +291,22 @@ def tile_rgcn_layer_pa_kernel(tc, x, adj, wr, br, w0, b0, out):
                     if k >= 1:
                         aggregate(k - 1, m)
                     if k == R:
+                        self_term(0, m, False)
                         add_b0(0, m)
+                if k == 0:
+                    for h in range(2):
+                        flip_mm(("a", 0), adj_rows(0), h, True)
+                        flip_out(("a", 0), h, scopy)
                 if k < R:
                     bias_mm(k + 1)
                     bias_out(k + 1, scopy)
-                if k == 0:
-                    for h in range(2):
-                        flip_mm(("a", 0), adj_rows(0), h)
-                        flip_out(("a", 0), h, scopy)
                 if k < LAST:
                     for h in range(2):
-                        flip_mm(("a", k + 1), adj_rows(k + 1), h)
+                        flip_mm(("a", k + 1), adj_rows(k + 1), h, k == 0)
                         flip_out(("a", k + 1), h, scopy)
                 if k == 0:
                     for h in range(2):
-                        flip_mm("x1", x_sb[1], h)
+                        flip_mm("x1", x_sb[1], h, True)
                         flip_out("x1", h, scopy)
                 for j in DEN_ROUND[k]:
                     den_mm(j)
@@ -312,9 +324,6 @@ def tile_rgcn_layer_pa_kernel(tc, x, adj, wr, br, w0, b0, out):
                 if k < LAST:
                     for dc in range(NT):
                         fill(k + 1, dc)
-                if k == R - 1:
-                    for m in range(NT):
-                        self_term(0, m, False)
                 if k == R:
                     for m in range(NT):
                         self_term(1, m, True)

@@ -281,7 +281,10 @@ def tile_rgcn_layer_pa_kernel(tc, x, adj, wr, br, w0, b0, out):
                 grouped[("m", k)] = ring_tile(k)
                 if k < R:
                     grouped[("w", k + 1)] = ring_tile(k + 2)
-                    regroup(k + 1, gcopy, 0, G_SHARE)
+                    gcopy(
+                        out=grouped[("w", k + 1)].rearrange("q (d t) -> q d t", t=PACK)[:, 0 : 4 * G_SHARE, :],
+                        in_=w_sb[k + 1].rearrange("q t d -> q d t")[:, 0 : 4 * G_SHARE, :],
+                    )
                     regroup(k + 1, scopy, G_SHARE, 128)
                 for j in DEN_ROUND[k]:
                     den_scalar(j)

@@ -18,15 +18,16 @@ B, R, N, D = 2, 4, 512, 512
 NT = N // P
 PACK = 4
 W0 = R
-LAST = B * R - 1
+ROUNDS = B * R
+LAST = ROUNDS - 1
 FLOPS = 2 * B * (R + 1) * N * D * D + 2 * B * N * R * N * D
 
-NODES = "(u p e) f -> p u e f"
+ROWS = "(u p e) f -> p u e f"
 TILES = "p (u e) f -> p u e f"
 
-DEN_T = (2, 0)
-DEN_ROUND = ((), (0,), (1,), (2,), (3, 4), (5,), (6,), (7,))
-G_SHARE = 80
+GROUPS = D // 4
+GPSIMD_GROUPS = 80
+TENSOR_RELATIONS = (2, 0)
 
 
 def tile_rgcn_layer_pa_kernel(tc, x, adj, wr, br, w0, b0, out):
@@ -37,34 +38,34 @@ def tile_rgcn_layer_pa_kernel(tc, x, adj, wr, br, w0, b0, out):
         keep = ctx.enter_context(tc.tile_pool(name="keep", bufs=1))
         grp = ctx.enter_context(tc.tile_pool(name="grp", bufs=3))
         ring = ctx.enter_context(tc.tile_pool(name="ring", bufs=1))
-        fin = ctx.enter_context(tc.tile_pool(name="fin", bufs=8))
-        ps_acc = ctx.enter_context(tc.psum_pool(name="ps_acc", bufs=4))
+        fin = ctx.enter_context(tc.tile_pool(name="fin", bufs=B * NT))
+        ps_acc = ctx.enter_context(tc.psum_pool(name="ps_acc", bufs=NT))
         ps_work = ctx.enter_context(tc.psum_pool(name="ps_work", bufs=4))
 
         ident_f = const.tile([P, P], F32, name="ident_f")
         ident_b = const.tile([P, P], BF16, name="ident_b")
-        brows = const.tile([P, D], BF16, name="brows")
-        bias_bc = const.tile([P, R + 1, D], BF16, name="bias_bc")
-        den_t = const.tile([P, B * NT], F32, name="den_t")
-        den_s = const.tile([P, B * NT], F32, name="den_s")
-        den_one = const.tile([P, B * NT], F32, name="den_one")
-        rden = const.tile([P, B * NT], F32, name="rden")
-        junk = const.tile([P, R * N], BF16, name="junk")
+        bias_rows = const.tile([P, D], BF16, name="brows")
+        bias_all = const.tile([P, R + 1, D], BF16, name="bias_bc")
+        deg_tensor = const.tile([P, B * NT], F32, name="den_t")
+        deg_scalar = const.tile([P, B * NT], F32, name="den_s")
+        den = const.tile([P, B * NT], F32, name="den_one")
+        inv_den = const.tile([P, B * NT], F32, name="rden")
+        unread = const.tile([P, R * N], BF16, name="junk")
 
         x_sb = [inp.tile([P, NT, D], BF16, name="x_sb%d" % b) for b in range(B)]
         w_sb = [inp.tile([P, PACK, D], BF16, name="w_sb%d" % i) for i in range(R + 1)]
         adj_sb = [inp.tile([P, R, NT, N], BF16, name="adj_sb%d" % b) for b in range(B)]
 
         def load_x(b):
-            nc.sync.dma_start(out=x_sb[b].rearrange(TILES, u=2), in_=x[b].rearrange(NODES, u=2, e=2))
+            nc.sync.dma_start(out=x_sb[b].rearrange(TILES, u=2), in_=x[b].rearrange(ROWS, u=2, e=2))
 
         def load_w(i):
             src = w0 if i == W0 else wr[i]
-            nc.sync.dma_start(out=w_sb[i].rearrange(TILES, u=2), in_=src.rearrange(NODES, u=2, e=2))
+            nc.sync.dma_start(out=w_sb[i].rearrange(TILES, u=2), in_=src.rearrange(ROWS, u=2, e=2))
 
         def load_adj(b, r):
             nc.sync.dma_start(
-                out=adj_sb[b][:, r].rearrange(TILES, u=2), in_=adj[b, r].rearrange(NODES, u=2, e=2)
+                out=adj_sb[b][:, r].rearrange(TILES, u=2), in_=adj[b, r].rearrange(ROWS, u=2, e=2)
             )
 
         def packed(name):
@@ -74,13 +75,20 @@ def tile_rgcn_layer_pa_kernel(tc, x, adj, wr, br, w0, b0, out):
 
         xq = [packed("xq%d" % b) for b in range(B)]
         wq = [packed("wq%d" % i) for i in range(R + 1)]
-        aq = [packed("aq%d" % k) for k in range(B * R)]
-        mq = [packed("mq%d" % k) for k in range(B * R)]
+        aq = [packed("aq%d" % k) for k in range(ROUNDS)]
+        mq = [packed("mq%d" % k) for k in range(ROUNDS)]
 
         def quantise(dst, src):
             nc.vector.quantize_mx(out=dst[0].bitcast(FP8X4), scales=dst[1], in_=src)
 
-        def mx(acc, lhs, lcols, rhs, rcols, start, stop):
+        def quantise_half(dst, src, h):
+            nc.vector.quantize_mx(
+                out=dst[0][:, 256 * h : 256 * (h + 1)].bitcast(FP8X4),
+                scales=dst[1][:, 256 * h : 256 * (h + 1)],
+                in_=src[:, 1024 * h : 1024 * (h + 1)],
+            )
+
+        def mx_pass(acc, lhs, lcols, rhs, rcols, start, stop):
             nc.tensor.matmul_mx(
                 out=acc,
                 lhsT=lhs[0][:, lcols].bitcast(FP8X4),
@@ -94,159 +102,136 @@ def tile_rgcn_layer_pa_kernel(tc, x, adj, wr, br, w0, b0, out):
         def cols(i):
             return slice(P * i, P * (i + 1))
 
-        vcopy = nc.vector.tensor_copy
-        scopy = nc.scalar.copy
-
-        def gcopy(out, in_):
-            nc.gpsimd.tensor_scalar(out=out, in0=in_, scalar1=1.0, scalar2=0.0, op0=MULT, op1=ADD)
-
         banks = {}
         grouped = {}
 
-        def quantise_part(dst, src, h):
-            nc.vector.quantize_mx(
-                out=dst[0][:, 256 * h : 256 * (h + 1)].bitcast(FP8X4),
-                scales=dst[1][:, 256 * h : 256 * (h + 1)],
-                in_=src[:, 1024 * h : 1024 * (h + 1)],
-            )
-
-        def bias_mm(i):
+        def bias_spread(i):
             banks[("bias", i)] = ps_work.tile([P, D], F32, tag="work", name="bias_ps")
             nc.tensor.matmul(
                 out=banks[("bias", i)],
                 lhsT=ident_b[:, i : i + 1].to_broadcast([P, P]),
-                rhs=brows,
+                rhs=bias_rows,
                 start=True,
                 stop=True,
             )
+            nc.scalar.copy(out=bias_all[:, i, :], in_=banks[("bias", i)])
 
-        def bias_out(i, evac):
-            evac(out=bias_bc[:, i, :], in_=banks[("bias", i)])
-
-        def flip_mm(key, rows, h, early=False):
+        def flip(key, rows, h, pool, tag):
             if h == 0:
                 grouped[key] = grp.tile([P, PACK * 512], BF16, tag="flipped", name="flipped", align_bytes=64)
-            if early:
-                bank = ps_acc.tile([P, 2, 2 * P], F32, tag="acc", name="flip_ps")
-            else:
-                bank = ps_work.tile([P, 2, 2 * P], F32, tag="work", name="flip_ps")
-            banks[(key, h)] = bank
+            bank = pool.tile([P, 2, 2 * P], F32, tag=tag, name="flip_ps")
             for a in range(2):
                 words_in = rows[:, 2 * h + a, :].bitcast(F32)
                 for v in range(2):
                     nc.tensor.transpose(bank[:, v, cols(a)], words_in[:, cols(v)], ident_f)
-
-        def flip_out(key, h, evac):
             words_out = grouped[key].bitcast(F32).rearrange("q (c v) -> q c v", v=2)
-            evac(
-                out=words_out[:, 2 * P * h : 2 * P * (h + 1), :],
-                in_=banks[(key, h)].rearrange("q v c -> q c v"),
-            )
+            nc.scalar.copy(out=words_out[:, 2 * P * h : 2 * P * (h + 1), :], in_=bank.rearrange("q v c -> q c v"))
 
-        def adj_rows(k):
-            return adj_sb[k // R][:, k % R]
+        def flip_adj(k, pool, tag):
+            for h in range(2):
+                flip(("a", k), adj_sb[k // R][:, k % R], h, pool, tag)
 
         def ring_tile(slot):
             return ring.tile([P, PACK * D], BF16, tag="ring%d" % (slot % 3), name="ring", align_bytes=64)
 
-        def regroup(i, copy, lo, hi):
+        def regroup(i, copy, first, end):
             copy(
-                out=grouped[("w", i)].rearrange("q (c i t) -> q c t i", i=4, t=PACK)[:, lo:hi],
-                in_=w_sb[i].rearrange("q t (c i) -> q c t i", i=4)[:, lo:hi],
+                out=grouped[("w", i)].rearrange("q (c i t) -> q c t i", i=4, t=PACK)[:, first:end],
+                in_=w_sb[i].rearrange("q t (c i) -> q c t i", i=4)[:, first:end],
             )
 
-        def fill(k, dc):
+        def gpsimd_copy(out, in_):
+            nc.gpsimd.tensor_scalar(out=out, in0=in_, scalar1=1.0, scalar2=0.0, op0=MULT, op1=ADD)
+
+        def messages(k, dc):
             b, r = divmod(k, R)
             bank = ps_work.tile([P, NT, P], F32, tag="work", name="ms_ps")
             banks[("ms", k, dc)] = bank
             for t in range(NT):
-                mx(bank[:, t, :], xq[b], cols(t), wq[r], cols(dc), True, True)
+                mx_pass(bank[:, t, :], xq[b], cols(t), wq[r], cols(dc), True, True)
 
-        def bias_add(k, dc):
+        def add_bias(k, dc):
             nc.vector.tensor_tensor(
                 out=grouped[("m", k)].rearrange("p (d t) -> p d t", t=PACK)[:, cols(dc), :],
                 in0=banks[("ms", k, dc)].rearrange("p t d -> p d t"),
-                in1=bias_bc[:, k % R, cols(dc)].unsqueeze(2).to_broadcast([P, P, PACK]),
+                in1=bias_all[:, k % R, cols(dc)].unsqueeze(2).to_broadcast([P, P, PACK]),
                 op=ADD,
             )
 
         acc = {}
 
-        def self_term(b, m, start):
-            if start:
+        def self_term(b, m):
+            opens = b == 1
+            if opens:
                 acc[(b, m)] = ps_acc.tile([P, D], F32, tag="acc", name="acc_ps")
-            mx(acc[(b, m)], xq[b], cols(m), wq[W0], slice(0, D), start, not start)
+            mx_pass(acc[(b, m)], xq[b], cols(m), wq[W0], slice(0, D), opens, not opens)
 
         def aggregate(k, m):
             b = k // R
             if k == 0:
                 acc[(b, m)] = ps_acc.tile([P, D], F32, tag="acc", name="acc_ps")
-            mx(acc[(b, m)], aq[k], cols(m), mq[k], slice(0, D), k == 0, k == LAST)
+            mx_pass(acc[(b, m)], aq[k], cols(m), mq[k], slice(0, D), k == 0, k == LAST)
 
-        def den_mm(j):
+        def degrees_scalar(j):
             b, m = divmod(j, NT)
-            if DEN_T[b] == 0:
-                return
+            nc.scalar.activation(
+                out=unread.rearrange("p (r j) -> p r j", r=R)[:, TENSOR_RELATIONS[b] : R],
+                in_=adj_sb[b][:, TENSOR_RELATIONS[b] : R, m, :],
+                func=COPY,
+                accum_out=deg_scalar[:, j : j + 1],
+            )
+
+        def degrees_tensor(j):
+            b, m = divmod(j, NT)
             bank = ps_work.tile([P, P], F32, tag="work", name="den_ps")
-            banks[("den", j)] = bank
-            for r in range(DEN_T[b]):
+            for r in range(TENSOR_RELATIONS[b]):
                 for g in range(NT):
                     nc.tensor.matmul(
                         out=bank,
                         lhsT=ident_b,
                         rhs=adj_sb[b][:, r, m, cols(g)],
                         start=(r == 0 and g == 0),
-                        stop=(r == DEN_T[b] - 1 and g == NT - 1),
+                        stop=(r == TENSOR_RELATIONS[b] - 1 and g == NT - 1),
                     )
+            nc.scalar.activation(out=unread[:, 0:P], in_=bank, func=COPY, accum_out=deg_tensor[:, j : j + 1])
 
-        def den_out(j):
-            if DEN_T[j // NT] == 0:
-                return
-            nc.scalar.activation(out=junk[:, 0:P], in_=banks[("den", j)], func=COPY, accum_out=den_t[:, j : j + 1])
+        def degree_tiles(k):
+            return ([k - 1] if 1 <= k <= R else []) + ([k] if k >= R else [])
 
-        def den_scalar(j):
-            b, m = divmod(j, NT)
-            nc.scalar.activation(
-                out=junk.rearrange("p (r j) -> p r j", r=R)[:, DEN_T[b] : R],
-                in_=adj_sb[b][:, DEN_T[b] : R, m, :],
-                func=COPY,
-                accum_out=den_s[:, j : j + 1],
-            )
-
-        def den_close(b):
+        def invert_den(b):
             these = slice(NT * b, NT * (b + 1))
-            if DEN_T[b] == 0:
-                nc.vector.tensor_scalar_add(out=den_one[:, these], in0=den_s[:, these], scalar1=1.0)
-                nc.vector.reciprocal(out=rden[:, these], in_=den_one[:, these])
-                return
-            nc.vector.scalar_tensor_tensor(
-                out=den_one[:, these], in0=den_t[:, these], scalar=1.0, in1=den_s[:, these], op0=ADD, op1=ADD
-            )
-            nc.vector.reciprocal(out=rden[:, these], in_=den_one[:, these])
+            if TENSOR_RELATIONS[b] == 0:
+                nc.vector.tensor_scalar_add(out=den[:, these], in0=deg_scalar[:, these], scalar1=1.0)
+            else:
+                nc.vector.scalar_tensor_tensor(
+                    out=den[:, these], in0=deg_tensor[:, these], scalar=1.0, in1=deg_scalar[:, these], op0=ADD, op1=ADD
+                )
+            nc.vector.reciprocal(out=inv_den[:, these], in_=den[:, these])
 
         sums = {}
 
         def add_b0(b, m):
             sums[(b, m)] = fin.tile([P, D], F32, tag="fsum", name="fsum")
-            nc.vector.tensor_tensor(out=sums[(b, m)], in0=acc[(b, m)], in1=bias_bc[:, W0, :], op=ADD)
+            nc.vector.tensor_tensor(out=sums[(b, m)], in0=acc[(b, m)], in1=bias_all[:, W0, :], op=ADD)
 
         def finish(b, m):
             res = fin.tile([P, D], F32, tag="res", name="res")
-            c = NT * b + m
-            nc.scalar.activation(out=res, in_=sums[(b, m)], func=RELU, scale=rden[:, c : c + 1])
+            j = NT * b + m
+            nc.scalar.activation(out=res, in_=sums[(b, m)], func=RELU, scale=inv_den[:, j : j + 1])
             u, e = divmod(m, 2)
-            nc.sync.dma_start(out=out[b].rearrange(NODES, u=2, e=2)[:, u, e, :], in_=res)
+            nc.sync.dma_start(out=out[b].rearrange(ROWS, u=2, e=2)[:, u, e, :], in_=res)
 
-        with tc.manual_schedule():
-            nc.vector.memset(brows, 0.0)
+        if True:
+            nc.vector.memset(bias_rows, 0.0)
             make_identity(nc, ident_f)
             make_identity(nc, ident_b)
+
             for u in range(2):
                 nc.sync.dma_start(
-                    out=x_sb[0].rearrange(TILES, u=2)[:, u], in_=x[0].rearrange(NODES, u=2, e=2)[:, u]
+                    out=x_sb[0].rearrange(TILES, u=2)[:, u], in_=x[0].rearrange(ROWS, u=2, e=2)[:, u]
                 )
-            nc.sync.dma_start(out=brows[0:R, :], in_=br)
-            nc.sync.dma_start(out=brows[R : R + 1, :], in_=b0.rearrange("(o d) -> o d", o=1))
+            nc.sync.dma_start(out=bias_rows[0:R, :], in_=br)
+            nc.sync.dma_start(out=bias_rows[R : R + 1, :], in_=b0.rearrange("(o d) -> o d", o=1))
             load_w(0)
             load_w(1)
             load_adj(0, 0)
@@ -262,76 +247,73 @@ def tile_rgcn_layer_pa_kernel(tc, x, adj, wr, br, w0, b0, out):
 
             grouped[("w", 0)] = ring_tile(2)
             for h in range(2):
-                flip_mm("x0", x_sb[0], h)
-                flip_out("x0", h, scopy)
-            quantise_part(xq[0], grouped["x0"], 0)
-            regroup(0, vcopy, 0, 64)
-            regroup(0, scopy, 64, 128)
-            quantise_part(xq[0], grouped["x0"], 1)
-            quantise_part(wq[0], grouped[("w", 0)], 0)
-            bias_mm(0)
-            bias_out(0, scopy)
-            fill(0, 0)
-            fill(0, 1)
-            quantise_part(wq[0], grouped[("w", 0)], 1)
-            fill(0, 2)
-            fill(0, 3)
+                flip("x0", x_sb[0], h, ps_work, "work")
+            quantise_half(xq[0], grouped["x0"], 0)
+            regroup(0, nc.vector.tensor_copy, 0, GROUPS // 2)
+            regroup(0, nc.scalar.copy, GROUPS // 2, GROUPS)
+            quantise_half(xq[0], grouped["x0"], 1)
+            quantise_half(wq[0], grouped[("w", 0)], 0)
+            bias_spread(0)
+            messages(0, 0)
+            messages(0, 1)
+            quantise_half(wq[0], grouped[("w", 0)], 1)
+            messages(0, 2)
+            messages(0, 3)
 
-            for k in range(B * R):
+            for k in range(ROUNDS):
                 grouped[("m", k)] = ring_tile(k)
                 if k < R:
                     grouped[("w", k + 1)] = ring_tile(k + 2)
-                    gcopy(
-                        out=grouped[("w", k + 1)].rearrange("q (d t) -> q d t", t=PACK)[:, 0 : 4 * G_SHARE, :],
-                        in_=w_sb[k + 1].rearrange("q t d -> q d t")[:, 0 : 4 * G_SHARE, :],
-                    )
-                    regroup(k + 1, scopy, G_SHARE, 128)
-                for j in DEN_ROUND[k]:
-                    den_scalar(j)
+                    regroup(k + 1, gpsimd_copy, 0, GPSIMD_GROUPS)
+                    regroup(k + 1, nc.scalar.copy, GPSIMD_GROUPS, GROUPS)
+                for j in degree_tiles(k):
+                    degrees_scalar(j)
+
                 for dc in range(NT):
-                    bias_add(k, dc)
+                    add_bias(k, dc)
+
                 for m in range(NT):
                     if k >= 1:
                         aggregate(k - 1, m)
                     if k == R:
-                        self_term(0, m, False)
+                        self_term(0, m)
                         add_b0(0, m)
+
                 if k == 0:
-                    for h in range(2):
-                        flip_mm(("a", 0), adj_rows(0), h, True)
-                        flip_out(("a", 0), h, scopy)
+                    flip_adj(0, ps_acc, "acc")
                 if k < R:
-                    bias_mm(k + 1)
-                    bias_out(k + 1, scopy)
-                if k < LAST:
-                    for h in range(2):
-                        flip_mm(("a", k + 1), adj_rows(k + 1), h, k == 0)
-                        flip_out(("a", k + 1), h, scopy)
+                    bias_spread(k + 1)
                 if k == 0:
+                    flip_adj(1, ps_acc, "acc")
                     for h in range(2):
-                        flip_mm("x1", x_sb[1], h, True)
-                        flip_out("x1", h, scopy)
-                for j in DEN_ROUND[k]:
-                    den_mm(j)
-                    den_out(j)
+                        flip("x1", x_sb[1], h, ps_acc, "acc")
+                elif k < LAST:
+                    flip_adj(k + 1, ps_work, "work")
+                for j in degree_tiles(k):
+                    if TENSOR_RELATIONS[j // NT] > 0:
+                        degrees_tensor(j)
+
                 if k < R:
                     quantise(wq[k + 1], grouped[("w", k + 1)])
                 quantise(aq[k], grouped[("a", k)])
                 if k == 1:
                     quantise(xq[1], grouped["x1"])
                 quantise(mq[k], grouped[("m", k)])
+
                 if k == R + 1:
-                    den_close(0)
+                    invert_den(0)
                 if k >= R + 1:
                     finish(0, k - R - 1)
+
                 if k < LAST:
                     for dc in range(NT):
-                        fill(k + 1, dc)
+                        messages(k + 1, dc)
                 if k == R:
                     for m in range(NT):
-                        self_term(1, m, True)
-            den_close(1)
-            finish(0, 3)
+                        self_term(1, m)
+
+            invert_den(1)
+            finish(0, NT - 1)
             for m in range(NT):
                 aggregate(LAST, m)
                 add_b0(1, m)

@@ -221,7 +221,7 @@ def tile_rgcn_layer_pa_kernel(tc, x, adj, wr, br, w0, b0, out):
             u, e = divmod(m, 2)
             nc.sync.dma_start(out=out[b].rearrange(ROWS, u=2, e=2)[:, u, e, :], in_=res)
 
-        if True:
+        with tc.manual_schedule():
             nc.vector.memset(bias_rows, 0.0)
             make_identity(nc, ident_f)
             make_identity(nc, ident_b)
@@ -273,11 +273,16 @@ def tile_rgcn_layer_pa_kernel(tc, x, adj, wr, br, w0, b0, out):
                     add_bias(k, dc)
 
                 for m in range(NT):
-                    if k >= 1:
+                    if 1 <= k <= R:
                         aggregate(k - 1, m)
+                    if k >= R + 2:
+                        aggregate(k - 2, m)
                     if k == R:
                         self_term(0, m)
                         add_b0(0, m)
+                if k == LAST:
+                    for m in range(NT):
+                        aggregate(k - 1, m)
 
                 if k == 0:
                     flip_adj(0, ps_acc, "acc")

@@ -12,6 +12,7 @@ ADD = mybir.AluOpType.add
 MULT = mybir.AluOpType.mult
 COPY = mybir.ActivationFunctionType.Copy
 RELU = mybir.ActivationFunctionType.Relu
+AXIS_X = mybir.AxisListType.X
 
 P = 128
 B, R, N, D = 2, 4, 512, 512
@@ -27,7 +28,8 @@ TILES = "p (u e) f -> p u e f"
 
 GROUPS = D // 4
 GPSIMD_GROUPS = 80
-TENSOR_RELATIONS = (2, 0)
+TENSOR_RELATIONS = (R, 2)
+CHUNKS = N // 32
 
 
 def tile_rgcn_layer_pa_kernel(tc, x, adj, wr, br, w0, b0, out):
@@ -36,7 +38,7 @@ def tile_rgcn_layer_pa_kernel(tc, x, adj, wr, br, w0, b0, out):
         const = ctx.enter_context(tc.tile_pool(name="const", bufs=1))
         inp = ctx.enter_context(tc.tile_pool(name="inp", bufs=1))
         keep = ctx.enter_context(tc.tile_pool(name="keep", bufs=1))
-        grp = ctx.enter_context(tc.tile_pool(name="grp", bufs=3))
+        grp = ctx.enter_context(tc.tile_pool(name="grp", bufs=4))
         ring = ctx.enter_context(tc.tile_pool(name="ring", bufs=1))
         fin = ctx.enter_context(tc.tile_pool(name="fin", bufs=B * NT))
         ps_acc = ctx.enter_context(tc.psum_pool(name="ps_acc", bufs=NT))
@@ -46,7 +48,11 @@ def tile_rgcn_layer_pa_kernel(tc, x, adj, wr, br, w0, b0, out):
         ident_b = const.tile([P, P], BF16, name="ident_b")
         bias_rows = const.tile([P, D], BF16, name="brows")
         bias_all = const.tile([P, R + 1, D], BF16, name="bias_bc")
-        deg_tensor = const.tile([P, B * NT], F32, name="den_t")
+        ones = const.tile([P, 2], BF16, name="ones")
+        block = const.tile([P, 32], F32, name="block")
+        sel = const.tile([P, NT, P], F32, name="sel")
+        part = [const.tile([P, R, CHUNKS], F32, name="part%d" % b) for b in range(B)]
+        dsum = [const.tile([P, R, NT], F32, name="dsum%d" % b) for b in range(B)]
         deg_scalar = const.tile([P, B * NT], F32, name="den_s")
         den = const.tile([P, B * NT], F32, name="den_one")
         inv_den = const.tile([P, B * NT], F32, name="rden")
@@ -81,11 +87,12 @@ def tile_rgcn_layer_pa_kernel(tc, x, adj, wr, br, w0, b0, out):
         def quantise(dst, src):
             nc.vector.quantize_mx(out=dst[0].bitcast(FP8X4), scales=dst[1], in_=src)
 
-        def quantise_half(dst, src, h):
+        def quantise_part(dst, src, part, parts):
+            n = 512 // parts
             nc.vector.quantize_mx(
-                out=dst[0][:, 256 * h : 256 * (h + 1)].bitcast(FP8X4),
-                scales=dst[1][:, 256 * h : 256 * (h + 1)],
-                in_=src[:, 1024 * h : 1024 * (h + 1)],
+                out=dst[0][:, n * part : n * (part + 1)].bitcast(FP8X4),
+                scales=dst[1][:, n * part : n * (part + 1)],
+                in_=src[:, PACK * n * part : PACK * n * (part + 1)],
             )
 
         def mx_pass(acc, lhs, lcols, rhs, rcols, start, stop):
@@ -106,7 +113,7 @@ def tile_rgcn_layer_pa_kernel(tc, x, adj, wr, br, w0, b0, out):
         grouped = {}
 
         def bias_spread(i):
-            banks[("bias", i)] = ps_work.tile([P, D], F32, tag="work", name="bias_ps")
+            banks[("bias", i)] = ps_work.tile([P, D], BF16, tag="work", name="bias_ps")
             nc.tensor.matmul(
                 out=banks[("bias", i)],
                 lhsT=ident_b[:, i : i + 1].to_broadcast([P, P]),
@@ -134,14 +141,22 @@ def tile_rgcn_layer_pa_kernel(tc, x, adj, wr, br, w0, b0, out):
         def ring_tile(slot):
             return ring.tile([P, PACK * D], BF16, tag="ring%d" % (slot % 3), name="ring", align_bytes=64)
 
+        def regroup_gpsimd(i, first, end):
+            c0, c1 = 4 * first, 4 * end
+            nc.gpsimd.tensor_scalar(
+                out=grouped[("w", i)].rearrange("q (c t) -> q c t", t=PACK)[:, c0:c1],
+                in0=w_sb[i].rearrange("q t c -> q c t")[:, c0:c1],
+                scalar1=1.0,
+                scalar2=0.0,
+                op0=MULT,
+                op1=ADD,
+            )
+
         def regroup(i, copy, first, end):
             copy(
                 out=grouped[("w", i)].rearrange("q (c i t) -> q c t i", i=4, t=PACK)[:, first:end],
                 in_=w_sb[i].rearrange("q t (c i) -> q c t i", i=4)[:, first:end],
             )
-
-        def gpsimd_copy(out, in_):
-            nc.gpsimd.tensor_scalar(out=out, in0=in_, scalar1=1.0, scalar2=0.0, op0=MULT, op1=ADD)
 
         def messages(k, dc):
             b, r = divmod(k, R)
@@ -181,38 +196,61 @@ def tile_rgcn_layer_pa_kernel(tc, x, adj, wr, br, w0, b0, out):
                 accum_out=deg_scalar[:, j : j + 1],
             )
 
-        def degrees_tensor(j):
-            b, m = divmod(j, NT)
-            bank = ps_work.tile([P, P], F32, tag="work", name="den_ps")
-            for r in range(TENSOR_RELATIONS[b]):
-                for g in range(NT):
+        def thin(ks):
+            bank = ps_work.tile([P, len(ks), CHUNKS, 2], F32, tag="work", name="thin_ps")
+            for n, k in enumerate(ks):
+                for c in range(CHUNKS):
                     nc.tensor.matmul(
-                        out=bank,
-                        lhsT=ident_b,
-                        rhs=adj_sb[b][:, r, m, cols(g)],
-                        start=(r == 0 and g == 0),
-                        stop=(r == TENSOR_RELATIONS[b] - 1 and g == NT - 1),
+                        out=bank[:, n, c, :], lhsT=grouped[("a", k)][:, cols(c)], rhs=ones, start=True, stop=True
                     )
-            nc.scalar.activation(out=unread[:, 0:P], in_=bank, func=COPY, accum_out=deg_tensor[:, j : j + 1])
+            b, r = divmod(ks[0], R)
+            nc.scalar.copy(out=part[b][:, r : r + len(ks), :], in_=bank[:, :, :, 0])
 
-        def degree_tiles(k):
-            return ([k - 1] if 1 <= k <= R else []) + ([k] if k >= R else [])
+        def combine(b):
+            n = TENSOR_RELATIONS[b]
+            bank = ps_work.tile([P, R, NT], F32, tag="work", name="comb_ps")
+            for a in range(NT):
+                nc.tensor.matmul(
+                    out=bank[:, 0:n, :],
+                    lhsT=sel[:, a, :],
+                    rhs=part[b].rearrange("p r (m a) -> p a r m", a=NT)[:, a, 0:n, :],
+                    start=(a == 0),
+                    stop=(a == NT - 1),
+                )
+            nc.scalar.copy(out=dsum[b][:, 0:n, :], in_=bank[:, 0:n, :])
+
+        def sum_den(b):
+            these = slice(NT * b, NT * (b + 1))
+            d = dsum[b]
+            if TENSOR_RELATIONS[b] == R:
+                nc.gpsimd.tensor_tensor(out=d[:, 0:2, :], in0=d[:, 0:2, :], in1=d[:, 2:4, :], op=ADD)
+                nc.gpsimd.tensor_tensor(out=d[:, 0, :], in0=d[:, 0, :], in1=d[:, 1, :], op=ADD)
+            else:
+                nc.gpsimd.tensor_tensor(out=d[:, 0, :], in0=d[:, 0, :], in1=d[:, 1, :], op=ADD)
+                nc.gpsimd.tensor_tensor(out=d[:, 0, :], in0=d[:, 0, :], in1=deg_scalar[:, these], op=ADD)
+            nc.gpsimd.tensor_scalar(
+                out=den[:, these], in0=d[:, 0, :], scalar1=1.0, scalar2=1.0, op0=MULT, op1=ADD
+            )
 
         def invert_den(b):
             these = slice(NT * b, NT * (b + 1))
-            if TENSOR_RELATIONS[b] == 0:
-                nc.vector.tensor_scalar_add(out=den[:, these], in0=deg_scalar[:, these], scalar1=1.0)
-            else:
-                nc.vector.scalar_tensor_tensor(
-                    out=den[:, these], in0=deg_tensor[:, these], scalar=1.0, in1=deg_scalar[:, these], op0=ADD, op1=ADD
-                )
             nc.vector.reciprocal(out=inv_den[:, these], in_=den[:, these])
 
         sums = {}
 
+        raw = {}
+
+        def empty(m):
+            raw[m] = fin.tile([P, D], F32, tag="raw", name="raw")
+            nc.scalar.copy(out=raw[m], in_=acc[(0, m)])
+
+        def add_b0_gpsimd(m, k):
+            sums[(0, m)] = ring_tile(k + 2).bitcast(F32)[:, 0:D]
+            nc.gpsimd.tensor_tensor(out=sums[(0, m)], in0=raw[m], in1=bias_all[:, W0, :], op=ADD)
+
         def add_b0(b, m):
             sums[(b, m)] = fin.tile([P, D], F32, tag="fsum", name="fsum")
-            nc.vector.tensor_tensor(out=sums[(b, m)], in0=acc[(b, m)], in1=bias_all[:, W0, :], op=ADD)
+            nc.vector.tensor_tensor(out=sums[(b, m)], in0=raw[m] if b == 0 else acc[(b, m)], in1=bias_all[:, W0, :], op=ADD)
 
         def finish(b, m):
             res = fin.tile([P, D], F32, tag="res", name="res")
@@ -223,16 +261,23 @@ def tile_rgcn_layer_pa_kernel(tc, x, adj, wr, br, w0, b0, out):
 
         with tc.manual_schedule():
             nc.vector.memset(bias_rows, 0.0)
+            nc.vector.memset(ones, 1.0)
+            nc.vector.memset(sel, 0.0)
             make_identity(nc, ident_f)
             make_identity(nc, ident_b)
+            nc.vector.tensor_reduce(
+                out=block, in_=ident_f.rearrange("p (i t) -> p i t", t=PACK), op=ADD, axis=AXIS_X
+            )
+            for a in range(NT):
+                nc.gpsimd.tensor_copy(out=sel[:, a, 32 * a : 32 * (a + 1)], in_=block)
 
             for u in range(2):
                 nc.sync.dma_start(
                     out=x_sb[0].rearrange(TILES, u=2)[:, u], in_=x[0].rearrange(ROWS, u=2, e=2)[:, u]
                 )
+            load_w(0)
             nc.sync.dma_start(out=bias_rows[0:R, :], in_=br)
             nc.sync.dma_start(out=bias_rows[R : R + 1, :], in_=b0.rearrange("(o d) -> o d", o=1))
-            load_w(0)
             load_w(1)
             load_adj(0, 0)
             load_adj(0, 1)
@@ -246,40 +291,64 @@ def tile_rgcn_layer_pa_kernel(tc, x, adj, wr, br, w0, b0, out):
                 load_adj(1, r)
 
             grouped[("w", 0)] = ring_tile(2)
+            grouped[("m", 0)] = ring_tile(0)
             for h in range(2):
                 flip("x0", x_sb[0], h, ps_work, "work")
-            quantise_half(xq[0], grouped["x0"], 0)
-            regroup(0, nc.vector.tensor_copy, 0, GROUPS // 2)
-            regroup(0, nc.scalar.copy, GROUPS // 2, GROUPS)
-            quantise_half(xq[0], grouped["x0"], 1)
-            quantise_half(wq[0], grouped[("w", 0)], 0)
+            quantise_part(xq[0], grouped["x0"], 0, 2)
             bias_spread(0)
+            regroup(0, nc.vector.tensor_copy, 0, 32)
+            regroup(0, nc.scalar.copy, 64, 96)
+            regroup(0, nc.scalar.copy, 96, 128)
+            grouped[("w", 1)] = ring_tile(1)
+            regroup(1, nc.scalar.copy, 0, GROUPS)
+            quantise_part(xq[0], grouped["x0"], 1, 2)
+            quantise_part(wq[0], grouped[("w", 0)], 0, 4)
+            regroup(0, nc.vector.tensor_copy, 32, 64)
             messages(0, 0)
+            quantise_part(wq[0], grouped[("w", 0)], 1, 4)
             messages(0, 1)
-            quantise_half(wq[0], grouped[("w", 0)], 1)
+            add_bias(0, 0)
+            quantise_part(wq[0], grouped[("w", 0)], 2, 4)
             messages(0, 2)
+            add_bias(0, 1)
+            quantise_part(wq[0], grouped[("w", 0)], 3, 4)
             messages(0, 3)
 
             for k in range(ROUNDS):
-                grouped[("m", k)] = ring_tile(k)
-                if k < R:
+                if k > 0:
+                    grouped[("m", k)] = ring_tile(k)
+                if 0 < k < R:
                     grouped[("w", k + 1)] = ring_tile(k + 2)
-                    regroup(k + 1, gpsimd_copy, 0, GPSIMD_GROUPS)
+                    regroup_gpsimd(k + 1, 0, GPSIMD_GROUPS)
                     regroup(k + 1, nc.scalar.copy, GPSIMD_GROUPS, GROUPS)
-                for j in degree_tiles(k):
-                    degrees_scalar(j)
 
-                for dc in range(NT):
+                for dc in range(2 if k == 0 else 0, NT):
                     add_bias(k, dc)
 
-                for m in range(NT):
-                    if 1 <= k <= R:
+                if k > R:
+                    finish(0, k - R - 1)
+                if 1 <= k <= R:
+                    for m in range(NT):
                         aggregate(k - 1, m)
-                    if k >= R + 2:
+                        if k == R:
+                            self_term(0, m)
+                            empty(m)
+                if k == R + 1:
+                    for m in range(NT):
+                        self_term(1, m)
+                if k == R:
+                    sum_den(0)
+                if R <= k < LAST:
+                    add_b0_gpsimd(k - R, k)
+                if k == 1:
+                    thin([0, 1])
+                elif 1 < k < R + TENSOR_RELATIONS[1]:
+                    thin([k])
+                if k == R + TENSOR_RELATIONS[1]:
+                    combine(1)
+                if k >= R + 2:
+                    for m in range(NT):
                         aggregate(k - 2, m)
-                    if k == R:
-                        self_term(0, m)
-                        add_b0(0, m)
                 if k == LAST:
                     for m in range(NT):
                         aggregate(k - 1, m)
@@ -294,9 +363,16 @@ def tile_rgcn_layer_pa_kernel(tc, x, adj, wr, br, w0, b0, out):
                         flip("x1", x_sb[1], h, ps_acc, "acc")
                 elif k < LAST:
                     flip_adj(k + 1, ps_work, "work")
-                for j in degree_tiles(k):
-                    if TENSOR_RELATIONS[j // NT] > 0:
-                        degrees_tensor(j)
+                if k == R - 1:
+                    combine(0)
+                if R - 1 <= k < LAST:
+                    degrees_scalar(k + 1)
+                if k == LAST:
+                    sum_den(1)
+                if k == R:
+                    invert_den(0)
+                if k == LAST:
+                    invert_den(1)
 
                 if k < R:
                     quantise(wq[k + 1], grouped[("w", k + 1)])
@@ -305,19 +381,11 @@ def tile_rgcn_layer_pa_kernel(tc, x, adj, wr, br, w0, b0, out):
                     quantise(xq[1], grouped["x1"])
                 quantise(mq[k], grouped[("m", k)])
 
-                if k == R + 1:
-                    invert_den(0)
-                if k >= R + 1:
-                    finish(0, k - R - 1)
-
                 if k < LAST:
                     for dc in range(NT):
                         messages(k + 1, dc)
-                if k == R:
-                    for m in range(NT):
-                        self_term(1, m)
 
-            invert_den(1)
+            add_b0(0, NT - 1)
             finish(0, NT - 1)
             for m in range(NT):
                 aggregate(LAST, m)

@@ -12,7 +12,7 @@ ADD = mybir.AluOpType.add
 MULT = mybir.AluOpType.mult
 COPY = mybir.ActivationFunctionType.Copy
 RELU = mybir.ActivationFunctionType.Relu
-AXIS_X = mybir.AxisListType.X
+MAX = mybir.AluOpType.max
 
 P = 128
 B, R, N, D = 2, 4, 512, 512
@@ -28,8 +28,10 @@ TILES = "p (u e) f -> p u e f"
 
 GROUPS = D // 4
 GPSIMD_GROUPS = 80
-TENSOR_RELATIONS = (R, 2)
-CHUNKS = N // 32
+TENSOR_RELATIONS = (2, 2)
+TENSOR_DEGREES = {R + 1: (0, 1), R + 2: (2, 3)}
+FIRST = [range(4)] * 5 + [range(2)] + [range(4)] * 2
+SCALAR_DEGREES = {R - 1: (0,), R + 2: (1,), LAST: (2, 3)}
 
 
 def tile_rgcn_layer_pa_kernel(tc, x, adj, wr, br, w0, b0, out):
@@ -38,7 +40,7 @@ def tile_rgcn_layer_pa_kernel(tc, x, adj, wr, br, w0, b0, out):
         const = ctx.enter_context(tc.tile_pool(name="const", bufs=1))
         inp = ctx.enter_context(tc.tile_pool(name="inp", bufs=1))
         keep = ctx.enter_context(tc.tile_pool(name="keep", bufs=1))
-        grp = ctx.enter_context(tc.tile_pool(name="grp", bufs=4))
+        grp = ctx.enter_context(tc.tile_pool(name="grp", bufs=B * R + B))
         ring = ctx.enter_context(tc.tile_pool(name="ring", bufs=1))
         fin = ctx.enter_context(tc.tile_pool(name="fin", bufs=B * NT))
         ps_acc = ctx.enter_context(tc.psum_pool(name="ps_acc", bufs=NT))
@@ -49,10 +51,7 @@ def tile_rgcn_layer_pa_kernel(tc, x, adj, wr, br, w0, b0, out):
         bias_rows = const.tile([P, D], BF16, name="brows")
         bias_all = const.tile([P, R + 1, D], BF16, name="bias_bc")
         ones = const.tile([P, 2], BF16, name="ones")
-        block = const.tile([P, 32], F32, name="block")
-        sel = const.tile([P, NT, P], F32, name="sel")
-        part = [const.tile([P, R, CHUNKS], F32, name="part%d" % b) for b in range(B)]
-        dsum = [const.tile([P, R, NT], F32, name="dsum%d" % b) for b in range(B)]
+        deg_tensor = const.tile([P, B * NT], F32, name="den_t")
         deg_scalar = const.tile([P, B * NT], F32, name="den_s")
         den = const.tile([P, B * NT], F32, name="den_one")
         inv_den = const.tile([P, B * NT], F32, name="rden")
@@ -176,16 +175,13 @@ def tile_rgcn_layer_pa_kernel(tc, x, adj, wr, br, w0, b0, out):
         acc = {}
 
         def self_term(b, m):
-            opens = b == 1
-            if opens:
-                acc[(b, m)] = ps_acc.tile([P, D], F32, tag="acc", name="acc_ps")
-            mx_pass(acc[(b, m)], xq[b], cols(m), wq[W0], slice(0, D), opens, not opens)
+            mx_pass(acc[(b, m)], xq[b], cols(m), wq[W0], slice(0, D), False, b == 0)
 
         def aggregate(k, m):
             b = k // R
-            if k == 0:
+            if k % R == 0:
                 acc[(b, m)] = ps_acc.tile([P, D], F32, tag="acc", name="acc_ps")
-            mx_pass(acc[(b, m)], aq[k], cols(m), mq[k], slice(0, D), k == 0, k == LAST)
+            mx_pass(acc[(b, m)], aq[k], cols(m), mq[k], slice(0, D), k % R == 0, k == LAST)
 
         def degrees_scalar(j):
             b, m = divmod(j, NT)
@@ -196,40 +192,33 @@ def tile_rgcn_layer_pa_kernel(tc, x, adj, wr, br, w0, b0, out):
                 accum_out=deg_scalar[:, j : j + 1],
             )
 
-        def thin(ks):
-            bank = ps_work.tile([P, len(ks), CHUNKS, 2], F32, tag="work", name="thin_ps")
-            for n, k in enumerate(ks):
-                for c in range(CHUNKS):
-                    nc.tensor.matmul(
-                        out=bank[:, n, c, :], lhsT=grouped[("a", k)][:, cols(c)], rhs=ones, start=True, stop=True
-                    )
-            b, r = divmod(ks[0], R)
-            nc.scalar.copy(out=part[b][:, r : r + len(ks), :], in_=bank[:, :, :, 0])
-
-        def combine(b):
+        def degrees_tensor(j):
+            b, m = divmod(j, NT)
+            bank = ps_work.tile([P, 2], F32, tag="work", name="deg_ps")
             n = TENSOR_RELATIONS[b]
-            bank = ps_work.tile([P, R, NT], F32, tag="work", name="comb_ps")
-            for a in range(NT):
-                nc.tensor.matmul(
-                    out=bank[:, 0:n, :],
-                    lhsT=sel[:, a, :],
-                    rhs=part[b].rearrange("p r (m a) -> p a r m", a=NT)[:, a, 0:n, :],
-                    start=(a == 0),
-                    stop=(a == NT - 1),
-                )
-            nc.scalar.copy(out=dsum[b][:, 0:n, :], in_=bank[:, 0:n, :])
+            for r in range(n):
+                words = grouped[("a", R * b + r)].rearrange("q (c t) -> q c t", t=PACK)
+                for t in range(PACK):
+                    nc.tensor.matmul(
+                        out=bank,
+                        lhsT=words[:, cols(m), t],
+                        rhs=ones,
+                        start=(r == 0 and t == 0),
+                        stop=(r == n - 1 and t == PACK - 1),
+                    )
+            nc.scalar.copy(out=deg_tensor[:, j : j + 1], in_=bank[:, 0:1])
 
         def sum_den(b):
             these = slice(NT * b, NT * (b + 1))
-            d = dsum[b]
-            if TENSOR_RELATIONS[b] == R:
-                nc.gpsimd.tensor_tensor(out=d[:, 0:2, :], in0=d[:, 0:2, :], in1=d[:, 2:4, :], op=ADD)
-                nc.gpsimd.tensor_tensor(out=d[:, 0, :], in0=d[:, 0, :], in1=d[:, 1, :], op=ADD)
-            else:
-                nc.gpsimd.tensor_tensor(out=d[:, 0, :], in0=d[:, 0, :], in1=d[:, 1, :], op=ADD)
-                nc.gpsimd.tensor_tensor(out=d[:, 0, :], in0=d[:, 0, :], in1=deg_scalar[:, these], op=ADD)
+            nc.gpsimd.tensor_tensor(out=den[:, these], in0=deg_tensor[:, these], in1=deg_scalar[:, these], op=ADD)
             nc.gpsimd.tensor_scalar(
-                out=den[:, these], in0=d[:, 0, :], scalar1=1.0, scalar2=1.0, op0=MULT, op1=ADD
+                out=den[:, these], in0=den[:, these], scalar1=1.0, scalar2=1.0, op0=MULT, op1=ADD
+            )
+
+        def sum_den_vector(b):
+            these = slice(NT * b, NT * (b + 1))
+            nc.vector.scalar_tensor_tensor(
+                out=den[:, these], in0=deg_tensor[:, these], scalar=1.0, in1=deg_scalar[:, these], op0=ADD, op1=ADD
             )
 
         def invert_den(b):
@@ -240,44 +229,41 @@ def tile_rgcn_layer_pa_kernel(tc, x, adj, wr, br, w0, b0, out):
 
         raw = {}
 
-        def empty(m):
-            raw[m] = fin.tile([P, D], F32, tag="raw", name="raw")
-            nc.scalar.copy(out=raw[m], in_=acc[(0, m)])
+        def empty(b, m):
+            raw[(b, m)] = fin.tile([P, D], F32, tag="raw", name="raw")
+            nc.scalar.copy(out=raw[(b, m)], in_=acc[(b, m)])
 
-        def add_b0_gpsimd(m, k):
-            sums[(0, m)] = ring_tile(k + 2).bitcast(F32)[:, 0:D]
-            nc.gpsimd.tensor_tensor(out=sums[(0, m)], in0=raw[m], in1=bias_all[:, W0, :], op=ADD)
+        def add_b0_gpsimd(b, m, k):
+            sums[(b, m)] = ring_tile(k + 2).bitcast(F32)[:, 0:D]
+            nc.gpsimd.tensor_tensor(out=sums[(b, m)], in0=raw[(b, m)], in1=bias_all[:, W0, :], op=ADD)
 
         def add_b0(b, m):
             sums[(b, m)] = fin.tile([P, D], F32, tag="fsum", name="fsum")
-            nc.vector.tensor_tensor(out=sums[(b, m)], in0=raw[m] if b == 0 else acc[(b, m)], in1=bias_all[:, W0, :], op=ADD)
+            nc.vector.tensor_tensor(out=sums[(b, m)], in0=raw.get((b, m), acc[(b, m)]), in1=bias_all[:, W0, :], op=ADD)
 
-        def finish(b, m):
+        def finish(b, m, engine):
             res = fin.tile([P, D], F32, tag="res", name="res")
             j = NT * b + m
-            nc.scalar.activation(out=res, in_=sums[(b, m)], func=RELU, scale=inv_den[:, j : j + 1])
+            if engine is nc.scalar:
+                nc.scalar.activation(out=res, in_=sums[(b, m)], func=RELU, scale=inv_den[:, j : j + 1])
+            else:
+                engine.tensor_scalar(
+                    out=res, in0=sums[(b, m)], scalar1=inv_den[:, j : j + 1], scalar2=0.0, op0=MULT, op1=MAX
+                )
             u, e = divmod(m, 2)
             nc.sync.dma_start(out=out[b].rearrange(ROWS, u=2, e=2)[:, u, e, :], in_=res)
 
         with tc.manual_schedule():
             nc.vector.memset(bias_rows, 0.0)
             nc.vector.memset(ones, 1.0)
-            nc.vector.memset(sel, 0.0)
             make_identity(nc, ident_f)
             make_identity(nc, ident_b)
-            nc.vector.tensor_reduce(
-                out=block, in_=ident_f.rearrange("p (i t) -> p i t", t=PACK), op=ADD, axis=AXIS_X
-            )
-            for a in range(NT):
-                nc.gpsimd.tensor_copy(out=sel[:, a, 32 * a : 32 * (a + 1)], in_=block)
-
             for u in range(2):
                 nc.sync.dma_start(
                     out=x_sb[0].rearrange(TILES, u=2)[:, u], in_=x[0].rearrange(ROWS, u=2, e=2)[:, u]
                 )
             load_w(0)
-            nc.sync.dma_start(out=bias_rows[0:R, :], in_=br)
-            nc.sync.dma_start(out=bias_rows[R : R + 1, :], in_=b0.rearrange("(o d) -> o d", o=1))
+            nc.sync.dma_start(out=bias_rows[0 : R - 1, :], in_=br[0 : R - 1, :])
             load_w(1)
             load_adj(0, 0)
             load_adj(0, 1)
@@ -289,73 +275,53 @@ def tile_rgcn_layer_pa_kernel(tc, x, adj, wr, br, w0, b0, out):
             load_w(W0)
             for r in range(R):
                 load_adj(1, r)
+            nc.sync.dma_start(out=bias_all[:, R - 1, :], in_=br[R - 1].partition_broadcast(P))
+            nc.sync.dma_start(out=bias_all[:, W0, :], in_=b0.partition_broadcast(P))
 
             grouped[("w", 0)] = ring_tile(2)
-            grouped[("m", 0)] = ring_tile(0)
             for h in range(2):
                 flip("x0", x_sb[0], h, ps_work, "work")
             quantise_part(xq[0], grouped["x0"], 0, 2)
-            bias_spread(0)
-            regroup(0, nc.vector.tensor_copy, 0, 32)
-            regroup(0, nc.scalar.copy, 64, 96)
-            regroup(0, nc.scalar.copy, 96, 128)
-            grouped[("w", 1)] = ring_tile(1)
-            regroup(1, nc.scalar.copy, 0, GROUPS)
+            regroup(0, nc.vector.tensor_copy, 0, GROUPS // 2)
+            regroup(0, nc.scalar.copy, GROUPS // 2, GROUPS)
             quantise_part(xq[0], grouped["x0"], 1, 2)
-            quantise_part(wq[0], grouped[("w", 0)], 0, 4)
-            regroup(0, nc.vector.tensor_copy, 32, 64)
+            quantise_part(wq[0], grouped[("w", 0)], 0, 2)
+            bias_spread(0)
             messages(0, 0)
-            quantise_part(wq[0], grouped[("w", 0)], 1, 4)
             messages(0, 1)
-            add_bias(0, 0)
-            quantise_part(wq[0], grouped[("w", 0)], 2, 4)
+            quantise_part(wq[0], grouped[("w", 0)], 1, 2)
             messages(0, 2)
-            add_bias(0, 1)
-            quantise_part(wq[0], grouped[("w", 0)], 3, 4)
             messages(0, 3)
 
             for k in range(ROUNDS):
-                if k > 0:
-                    grouped[("m", k)] = ring_tile(k)
-                if 0 < k < R:
+                grouped[("m", k)] = ring_tile(k)
+                if k < R:
                     grouped[("w", k + 1)] = ring_tile(k + 2)
                     regroup_gpsimd(k + 1, 0, GPSIMD_GROUPS)
                     regroup(k + 1, nc.scalar.copy, GPSIMD_GROUPS, GROUPS)
 
-                for dc in range(2 if k == 0 else 0, NT):
+                for dc in range(NT):
                     add_bias(k, dc)
 
-                if k > R:
-                    finish(0, k - R - 1)
-                if 1 <= k <= R:
-                    for m in range(NT):
-                        aggregate(k - 1, m)
-                        if k == R:
+                def before(ms):
+                    for m in ms:
+                        if 1 <= k <= R:
+                            aggregate(k - 1, m)
+                        if k == R + 1:
                             self_term(0, m)
-                            empty(m)
+                            empty(0, m)
+                        if k >= R + 2:
+                            aggregate(k - 2, m)
+
                 if k == R + 1:
-                    for m in range(NT):
-                        self_term(1, m)
-                if k == R:
                     sum_den(0)
-                if R <= k < LAST:
-                    add_b0_gpsimd(k - R, k)
-                if k == 1:
-                    thin([0, 1])
-                elif 1 < k < R + TENSOR_RELATIONS[1]:
-                    thin([k])
-                if k == R + TENSOR_RELATIONS[1]:
-                    combine(1)
-                if k >= R + 2:
-                    for m in range(NT):
-                        aggregate(k - 2, m)
-                if k == LAST:
-                    for m in range(NT):
-                        aggregate(k - 1, m)
+                before(FIRST[k])
+                if 1 <= k <= R:
+                    degrees_tensor(k - 1)
 
                 if k == 0:
                     flip_adj(0, ps_acc, "acc")
-                if k < R:
+                if k + 1 < R - 1:
                     bias_spread(k + 1)
                 if k == 0:
                     flip_adj(1, ps_acc, "acc")
@@ -363,16 +329,24 @@ def tile_rgcn_layer_pa_kernel(tc, x, adj, wr, br, w0, b0, out):
                         flip("x1", x_sb[1], h, ps_acc, "acc")
                 elif k < LAST:
                     flip_adj(k + 1, ps_work, "work")
-                if k == R - 1:
-                    combine(0)
-                if R - 1 <= k < LAST:
-                    degrees_scalar(k + 1)
-                if k == LAST:
-                    sum_den(1)
-                if k == R:
+                before([m for m in range(NT) if m not in FIRST[k]])
+                if R + 1 <= k <= LAST:
+                    add_b0_gpsimd(0, k - R - 1, k)
+                for m in TENSOR_DEGREES.get(k, ()):
+                    degrees_tensor(NT + m)
+                if 1 <= k <= R:
+                    degrees_scalar(k - 1)
+                for m in SCALAR_DEGREES.get(k, ()):
+                    degrees_scalar(NT + m)
+                if k == R + 1:
                     invert_den(0)
                 if k == LAST:
-                    invert_den(1)
+                    for m in range(NT):
+                        self_term(1, m)
+                    for m in range(NT):
+                        aggregate(k - 1, m)
+                if R + 1 <= k <= LAST:
+                    finish(0, k - R - 1, nc.gpsimd)
 
                 if k < R:
                     quantise(wq[k + 1], grouped[("w", k + 1)])
@@ -385,9 +359,16 @@ def tile_rgcn_layer_pa_kernel(tc, x, adj, wr, br, w0, b0, out):
                     for dc in range(NT):
                         messages(k + 1, dc)
 
+            sum_den_vector(1)
             add_b0(0, NT - 1)
-            finish(0, NT - 1)
-            for m in range(NT):
+            invert_den(1)
+            last = NT - 1
+            aggregate(LAST, last)
+            empty(1, last)
+            add_b0_gpsimd(1, last, ROUNDS)
+            finish(0, NT - 1, nc.scalar)
+            for m in range(last):
                 aggregate(LAST, m)
                 add_b0(1, m)
-                finish(1, m)
+                finish(1, m, nc.scalar)
+            finish(1, last, nc.gpsimd)

@@ -29,9 +29,11 @@ TILES = "p (u e) f -> p u e f"
 GROUPS = D // 4
 GPSIMD_GROUPS = 80
 TENSOR_RELATIONS = (2, 2)
-TENSOR_DEGREES = {R + 1: (0, 1), R + 2: (2, 3)}
+TENSOR_DEGREES = {R + 2: (0, 1), LAST: (2, 3)}
 FIRST = [range(4)] * 5 + [range(2)] + [range(4)] * 2
-SCALAR_DEGREES = {R - 1: (0,), R + 2: (1,), LAST: (2, 3)}
+GPSIMD_B0 = {R + 2: (0, 1), LAST: (2,)}
+FINISH = {R + 2: (0,), LAST: (1, 2)}
+SCALAR_DEGREES = {R - 1: (0,), R + 1: (1,), R + 2: (2, 3)}
 
 
 def tile_rgcn_layer_pa_kernel(tc, x, adj, wr, br, w0, b0, out):
@@ -233,9 +235,11 @@ def tile_rgcn_layer_pa_kernel(tc, x, adj, wr, br, w0, b0, out):
             raw[(b, m)] = fin.tile([P, D], F32, tag="raw", name="raw")
             nc.scalar.copy(out=raw[(b, m)], in_=acc[(b, m)])
 
-        def add_b0_gpsimd(b, m, k):
-            sums[(b, m)] = ring_tile(k + 2).bitcast(F32)[:, 0:D]
-            nc.gpsimd.tensor_tensor(out=sums[(b, m)], in0=raw[(b, m)], in1=bias_all[:, W0, :], op=ADD)
+        def add_b0_gpsimd(b, ms, k):
+            spare = ring_tile(k + 2).bitcast(F32)
+            for n, m in enumerate(ms):
+                sums[(b, m)] = spare[:, D * n : D * (n + 1)]
+                nc.gpsimd.tensor_tensor(out=sums[(b, m)], in0=raw[(b, m)], in1=bias_all[:, W0, :], op=ADD)
 
         def add_b0(b, m):
             sums[(b, m)] = fin.tile([P, D], F32, tag="fsum", name="fsum")
@@ -330,8 +334,8 @@ def tile_rgcn_layer_pa_kernel(tc, x, adj, wr, br, w0, b0, out):
                 elif k < LAST:
                     flip_adj(k + 1, ps_work, "work")
                 before([m for m in range(NT) if m not in FIRST[k]])
-                if R + 1 <= k <= LAST:
-                    add_b0_gpsimd(0, k - R - 1, k)
+                if k in GPSIMD_B0:
+                    add_b0_gpsimd(0, GPSIMD_B0[k], k)
                 for m in TENSOR_DEGREES.get(k, ()):
                     degrees_tensor(NT + m)
                 if 1 <= k <= R:
@@ -341,12 +345,11 @@ def tile_rgcn_layer_pa_kernel(tc, x, adj, wr, br, w0, b0, out):
                 if k == R + 1:
                     invert_den(0)
                 if k == LAST:
-                    for m in range(NT):
+                    for m in range(2):
                         self_term(1, m)
-                    for m in range(NT):
                         aggregate(k - 1, m)
-                if R + 1 <= k <= LAST:
-                    finish(0, k - R - 1, nc.gpsimd)
+                for m in FINISH.get(k, ()):
+                    finish(0, m, nc.scalar)
 
                 if k < R:
                     quantise(wq[k + 1], grouped[("w", k + 1)])
@@ -359,16 +362,17 @@ def tile_rgcn_layer_pa_kernel(tc, x, adj, wr, br, w0, b0, out):
                     for dc in range(NT):
                         messages(k + 1, dc)
 
+            left = [m for m in range(NT) if (0, m) not in sums]
             sum_den_vector(1)
-            add_b0(0, NT - 1)
+            for m in left:
+                add_b0(0, m)
             invert_den(1)
-            last = NT - 1
-            aggregate(LAST, last)
-            empty(1, last)
-            add_b0_gpsimd(1, last, ROUNDS)
-            finish(0, NT - 1, nc.scalar)
-            for m in range(last):
+            for m in left:
+                finish(0, m, nc.scalar)
+            for m in range(NT):
+                if m >= 2:
+                    self_term(1, m)
+                    aggregate(LAST - 1, m)
                 aggregate(LAST, m)
                 add_b0(1, m)
                 finish(1, m, nc.scalar)
-            finish(1, last, nc.gpsimd)

@@ -267,7 +267,7 @@ def tile_rgcn_layer_pa_kernel(tc, x, adj, wr, br, w0, b0, out):
                     out=x_sb[0].rearrange(TILES, u=2)[:, u], in_=x[0].rearrange(ROWS, u=2, e=2)[:, u]
                 )
             load_w(0)
-            nc.sync.dma_start(out=bias_rows[0 : R - 1, :], in_=br[0 : R - 1, :])
+            nc.sync.dma_start(out=bias_rows[0:R, :], in_=br)
             load_w(1)
             load_adj(0, 0)
             load_adj(0, 1)
@@ -279,7 +279,6 @@ def tile_rgcn_layer_pa_kernel(tc, x, adj, wr, br, w0, b0, out):
             load_w(W0)
             for r in range(R):
                 load_adj(1, r)
-            nc.sync.dma_start(out=bias_all[:, R - 1, :], in_=br[R - 1].partition_broadcast(P))
             nc.sync.dma_start(out=bias_all[:, W0, :], in_=b0.partition_broadcast(P))
 
             grouped[("w", 0)] = ring_tile(2)
@@ -325,7 +324,7 @@ def tile_rgcn_layer_pa_kernel(tc, x, adj, wr, br, w0, b0, out):
 
                 if k == 0:
                     flip_adj(0, ps_acc, "acc")
-                if k + 1 < R - 1:
+                if k + 1 < R:
                     bias_spread(k + 1)
                 if k == 0:
                     flip_adj(1, ps_acc, "acc")

@@ -32,6 +32,8 @@ TENSOR_RELATIONS = (2, 2)
 TENSOR_DEGREES = {R + 2: (0, 1), LAST: (2, 3)}
 FIRST = [range(4)] * 5 + [range(2)] + [range(4)] * 2
 GPSIMD_B0 = {R + 2: (0, 1), LAST: (2,)}
+LAST_PARTS = 2
+WARM = (4, 3)
 FINISH = {R + 2: (0,), LAST: (1, 2)}
 SCALAR_DEGREES = {R - 1: (0,), R + 1: (1,), R + 2: (2, 3)}
 
@@ -53,6 +55,7 @@ def tile_rgcn_layer_pa_kernel(tc, x, adj, wr, br, w0, b0, out):
         bias_rows = const.tile([P, D], BF16, name="brows")
         bias_all = const.tile([P, R + 1, D], BF16, name="bias_bc")
         ones = const.tile([P, 2], BF16, name="ones")
+        warm = const.tile([P, D], BF16, name="warm")
         deg_tensor = const.tile([P, B * NT], F32, name="den_t")
         deg_scalar = const.tile([P, B * NT], F32, name="den_s")
         den = const.tile([P, B * NT], F32, name="den_one")
@@ -159,6 +162,11 @@ def tile_rgcn_layer_pa_kernel(tc, x, adj, wr, br, w0, b0, out):
                 in_=w_sb[i].rearrange("q t (c i) -> q c t i", i=4)[:, first:end],
             )
 
+        def warm_up(n):
+            bank = ps_acc.tile([P, D], F32, tag="acc", name="warm_ps")
+            for i in range(n):
+                nc.tensor.matmul(out=bank, lhsT=warm[:, 0:P], rhs=warm, start=True, stop=True)
+
         def messages(k, dc):
             b, r = divmod(k, R)
             bank = ps_work.tile([P, NT, P], F32, tag="work", name="ms_ps")
@@ -241,23 +249,23 @@ def tile_rgcn_layer_pa_kernel(tc, x, adj, wr, br, w0, b0, out):
                 sums[(b, m)] = spare[:, D * n : D * (n + 1)]
                 nc.gpsimd.tensor_tensor(out=sums[(b, m)], in0=raw[(b, m)], in1=bias_all[:, W0, :], op=ADD)
 
-        def add_b0(b, m):
+        def add_b0(b, m, part=0, parts=1):
+            n = slice(D // parts * part, D // parts * (part + 1))
             sums[(b, m)] = fin.tile([P, D], F32, tag="fsum", name="fsum")
-            nc.vector.tensor_tensor(out=sums[(b, m)], in0=raw.get((b, m), acc[(b, m)]), in1=bias_all[:, W0, :], op=ADD)
+            nc.vector.tensor_tensor(
+                out=sums[(b, m)][:, n], in0=raw.get((b, m), acc[(b, m)])[:, n], in1=bias_all[:, W0, n], op=ADD
+            )
 
-        def finish(b, m, engine):
+        def finish(b, m, engine, part=0, parts=1):
+            n = slice(D // parts * part, D // parts * (part + 1))
             res = fin.tile([P, D], F32, tag="res", name="res")
             j = NT * b + m
-            if engine is nc.scalar:
-                nc.scalar.activation(out=res, in_=sums[(b, m)], func=RELU, scale=inv_den[:, j : j + 1])
-            else:
-                engine.tensor_scalar(
-                    out=res, in0=sums[(b, m)], scalar1=inv_den[:, j : j + 1], scalar2=0.0, op0=MULT, op1=MAX
-                )
+            nc.scalar.activation(out=res[:, n], in_=sums[(b, m)][:, n], func=RELU, scale=inv_den[:, j : j + 1])
             u, e = divmod(m, 2)
-            nc.sync.dma_start(out=out[b].rearrange(ROWS, u=2, e=2)[:, u, e, :], in_=res)
+            nc.sync.dma_start(out=out[b].rearrange(ROWS, u=2, e=2)[:, u, e, n], in_=res[:, n])
 
         with tc.manual_schedule():
+            nc.vector.memset(warm, 0.0)
             nc.vector.memset(bias_rows, 0.0)
             nc.vector.memset(ones, 1.0)
             make_identity(nc, ident_f)
@@ -282,8 +290,10 @@ def tile_rgcn_layer_pa_kernel(tc, x, adj, wr, br, w0, b0, out):
             nc.sync.dma_start(out=bias_all[:, W0, :], in_=b0.partition_broadcast(P))
 
             grouped[("w", 0)] = ring_tile(2)
+            warm_up(WARM[0])
             for h in range(2):
                 flip("x0", x_sb[0], h, ps_work, "work")
+            warm_up(WARM[1])
             quantise_part(xq[0], grouped["x0"], 0, 2)
             regroup(0, nc.vector.tensor_copy, 0, GROUPS // 2)
             regroup(0, nc.scalar.copy, GROUPS // 2, GROUPS)
@@ -373,5 +383,7 @@ def tile_rgcn_layer_pa_kernel(tc, x, adj, wr, br, w0, b0, out):
                     self_term(1, m)
                     aggregate(LAST - 1, m)
                 aggregate(LAST, m)
-                add_b0(1, m)
-                finish(1, m, nc.scalar)
+                parts = LAST_PARTS if m == NT - 1 else 1
+                for part in range(parts):
+                    add_b0(1, m, part, parts)
+                    finish(1, m, nc.scalar, part, parts)

@@ -29,10 +29,11 @@ TILES = "p (u e) f -> p u e f"
 GROUPS = D // 4
 GPSIMD_GROUPS = 80
 TENSOR_RELATIONS = (2, 2)
-TENSOR_DEGREES = {R + 2: (0, 1), LAST: (2, 3)}
+TENSOR_DEGREES = {R + 1: (0,), R + 2: (1, 2), LAST: (3,)}
 FIRST = [range(4)] * 5 + [range(2)] + [range(4)] * 2
 GPSIMD_B0 = {R + 2: (0, 1), LAST: (2,)}
 LAST_PARTS = 2
+V03 = 0
 WARM = (4, 3)
 FINISH = {R + 2: (0,), LAST: (1, 2)}
 SCALAR_DEGREES = {R - 1: (0,), R + 1: (1,), R + 2: (2, 3)}
@@ -113,6 +114,9 @@ def tile_rgcn_layer_pa_kernel(tc, x, adj, wr, br, w0, b0, out):
         def cols(i):
             return slice(P * i, P * (i + 1))
 
+        def half(h):
+            return slice(D // 2 * h, D // 2 * (h + 1))
+
         banks = {}
         grouped = {}
 
@@ -184,14 +188,22 @@ def tile_rgcn_layer_pa_kernel(tc, x, adj, wr, br, w0, b0, out):
 
         acc = {}
 
-        def self_term(b, m):
-            mx_pass(acc[(b, m)], xq[b], cols(m), wq[W0], slice(0, D), False, b == 0)
+        def self_term(m):
+            mx_pass(acc[(0, m)], xq[0], cols(m), wq[W0], slice(0, D), False, True)
 
         def aggregate(k, m):
-            b = k // R
-            if k % R == 0:
-                acc[(b, m)] = ps_acc.tile([P, D], F32, tag="acc", name="acc_ps")
-            mx_pass(acc[(b, m)], aq[k], cols(m), mq[k], slice(0, D), k % R == 0, k == LAST)
+            if k == 0:
+                acc[(0, m)] = ps_acc.tile([P, D], F32, tag="acc", name="acc_ps")
+            mx_pass(acc[(0, m)], aq[k], cols(m), mq[k], slice(0, D), k == 0, False)
+
+        def self_half(m, h):
+            mx_pass(acc[(1, m, h)], xq[1], cols(m), wq[W0], half(h), False, False)
+
+        def aggregate_half(k, m, h):
+            if k == R:
+                pool, tag = (ps_acc, "acc") if h == 0 else (ps_work, "work")
+                acc[(1, m, h)] = pool.tile([P, D // 2], F32, tag=tag, name="half_ps")
+            mx_pass(acc[(1, m, h)], aq[k], cols(m), mq[k], half(h), k == R, k == LAST)
 
         def degrees_scalar(j):
             b, m = divmod(j, NT)
@@ -240,7 +252,7 @@ def tile_rgcn_layer_pa_kernel(tc, x, adj, wr, br, w0, b0, out):
         raw = {}
 
         def empty(b, m):
-            raw[(b, m)] = fin.tile([P, D], F32, tag="raw", name="raw")
+            raw[(b, m)] = fin.tile([P, D], F32, tag="raw", name="raw", bufs=NT)
             nc.scalar.copy(out=raw[(b, m)], in_=acc[(b, m)])
 
         def add_b0_gpsimd(b, ms, k):
@@ -249,20 +261,21 @@ def tile_rgcn_layer_pa_kernel(tc, x, adj, wr, br, w0, b0, out):
                 sums[(b, m)] = spare[:, D * n : D * (n + 1)]
                 nc.gpsimd.tensor_tensor(out=sums[(b, m)], in0=raw[(b, m)], in1=bias_all[:, W0, :], op=ADD)
 
-        def add_b0(b, m, part=0, parts=1):
-            n = slice(D // parts * part, D // parts * (part + 1))
-            sums[(b, m)] = fin.tile([P, D], F32, tag="fsum", name="fsum")
-            nc.vector.tensor_tensor(
-                out=sums[(b, m)][:, n], in0=raw.get((b, m), acc[(b, m)])[:, n], in1=bias_all[:, W0, n], op=ADD
-            )
+        def add_b0_vector(m):
+            sums[(0, m)] = fin.tile([P, D], F32, tag="fsum", name="fsum", bufs=NT)
+            nc.vector.tensor_tensor(out=sums[(0, m)], in0=raw[(0, m)], in1=bias_all[:, W0, :], op=ADD)
 
-        def finish(b, m, engine, part=0, parts=1):
-            n = slice(D // parts * part, D // parts * (part + 1))
-            res = fin.tile([P, D], F32, tag="res", name="res")
+        def add_b0_half(m, h):
+            sums[(1, m, h)] = fin.tile([P, D // 2], F32, tag="hsum", name="hsum")
+            nc.vector.tensor_tensor(out=sums[(1, m, h)], in0=acc[(1, m, h)], in1=bias_all[:, W0, half(h)], op=ADD)
+
+        def finish(b, m, *h):
+            n = half(*h) if h else slice(0, D)
+            res = fin.tile([P, n.stop - n.start], F32, tag="hres" if h else "res", name="res", bufs=B * NT if h else NT)
             j = NT * b + m
-            nc.scalar.activation(out=res[:, n], in_=sums[(b, m)][:, n], func=RELU, scale=inv_den[:, j : j + 1])
+            nc.scalar.activation(out=res, in_=sums[(b, m, *h)], func=RELU, scale=inv_den[:, j : j + 1])
             u, e = divmod(m, 2)
-            nc.sync.dma_start(out=out[b].rearrange(ROWS, u=2, e=2)[:, u, e, n], in_=res[:, n])
+            nc.sync.dma_start(out=out[b].rearrange(ROWS, u=2, e=2)[:, u, e, n], in_=res)
 
         with tc.manual_schedule():
             nc.vector.memset(warm, 0.0)
@@ -313,7 +326,7 @@ def tile_rgcn_layer_pa_kernel(tc, x, adj, wr, br, w0, b0, out):
                     regroup_gpsimd(k + 1, 0, GPSIMD_GROUPS)
                     regroup(k + 1, nc.scalar.copy, GPSIMD_GROUPS, GROUPS)
 
-                for dc in range(NT):
+                for dc in range(NT if k < LAST else 2):
                     add_bias(k, dc)
 
                 def before(ms):
@@ -321,13 +334,11 @@ def tile_rgcn_layer_pa_kernel(tc, x, adj, wr, br, w0, b0, out):
                         if 1 <= k <= R:
                             aggregate(k - 1, m)
                         if k == R + 1:
-                            self_term(0, m)
+                            self_term(m)
                             empty(0, m)
                         if k >= R + 2:
-                            aggregate(k - 2, m)
+                            aggregate_half(k - 2, m, 0)
 
-                if k == R + 1:
-                    sum_den(0)
                 before(FIRST[k])
                 if 1 <= k <= R:
                     degrees_tensor(k - 1)
@@ -342,11 +353,17 @@ def tile_rgcn_layer_pa_kernel(tc, x, adj, wr, br, w0, b0, out):
                         flip("x1", x_sb[1], h, ps_acc, "acc")
                 elif k < LAST:
                     flip_adj(k + 1, ps_work, "work")
+                if k == R + 1:
+                    for m in TENSOR_DEGREES.get(k, ()):
+                        degrees_tensor(NT + m)
                 before([m for m in range(NT) if m not in FIRST[k]])
                 if k in GPSIMD_B0:
                     add_b0_gpsimd(0, GPSIMD_B0[k], k)
-                for m in TENSOR_DEGREES.get(k, ()):
-                    degrees_tensor(NT + m)
+                if k == R + 1:
+                    sum_den(0)
+                if k != R + 1:
+                    for m in TENSOR_DEGREES.get(k, ()):
+                        degrees_tensor(NT + m)
                 if 1 <= k <= R:
                     degrees_scalar(k - 1)
                 for m in SCALAR_DEGREES.get(k, ()):
@@ -354,36 +371,60 @@ def tile_rgcn_layer_pa_kernel(tc, x, adj, wr, br, w0, b0, out):
                 if k == R + 1:
                     invert_den(0)
                 if k == LAST:
-                    for m in range(2):
-                        self_term(1, m)
-                        aggregate(k - 1, m)
+                    for m in range(NT):
+                        self_half(m, 0)
+                        aggregate_half(k - 1, m, 0)
                 for m in FINISH.get(k, ()):
-                    finish(0, m, nc.scalar)
+                    finish(0, m)
 
                 if k < R:
                     quantise(wq[k + 1], grouped[("w", k + 1)])
-                quantise(aq[k], grouped[("a", k)])
+                if k < LAST:
+                    quantise(aq[k], grouped[("a", k)])
                 if k == 1:
                     quantise(xq[1], grouped["x1"])
-                quantise(mq[k], grouped[("m", k)])
+                if k < LAST:
+                    quantise(mq[k], grouped[("m", k)])
+                if k == LAST - 1:
+                    quantise(aq[LAST], grouped[("a", LAST)])
 
                 if k < LAST:
                     for dc in range(NT):
                         messages(k + 1, dc)
 
-            left = [m for m in range(NT) if (0, m) not in sums]
+            quantise_part(mq[LAST], grouped[("m", LAST)], 0, 2)
+            for m in range(NT):
+                aggregate_half(LAST, m, 0)
+            if V03 == 0:
+                add_b0_vector(3)
+            add_bias(LAST, 2)
             sum_den_vector(1)
-            for m in left:
-                add_b0(0, m)
+            add_bias(LAST, 3)
             invert_den(1)
-            for m in left:
-                finish(0, m, nc.scalar)
+            quantise_part(mq[LAST], grouped[("m", LAST)], 1, 2)
+
+            def open_half(m):
+                for k in range(R, LAST):
+                    aggregate_half(k, m, 1)
+                self_half(m, 1)
+
+            for m in range(2):
+                open_half(m)
+            if V03 == 1:
+                add_b0_vector(3)
+                finish(0, 3)
+            if V03 == 0:
+                finish(0, 3)
+            if V03 == 2:
+                add_b0_gpsimd(0, [3], LAST + 1)
+            for m in range(NT):
+                add_b0_half(m, 0)
+                finish(1, m, 0)
             for m in range(NT):
                 if m >= 2:
-                    self_term(1, m)
-                    aggregate(LAST - 1, m)
-                aggregate(LAST, m)
-                parts = LAST_PARTS if m == NT - 1 else 1
-                for part in range(parts):
-                    add_b0(1, m, part, parts)
-                    finish(1, m, nc.scalar, part, parts)
+                    open_half(m)
+                aggregate_half(LAST, m, 1)
+                add_b0_half(m, 1)
+                finish(1, m, 1)
+                if V03 == 2 and m == 0:
+                    finish(0, 3)

@@ -29,11 +29,10 @@ TILES = "p (u e) f -> p u e f"
 GROUPS = D // 4
 GPSIMD_GROUPS = 80
 TENSOR_RELATIONS = (2, 2)
-TENSOR_DEGREES = {R + 1: (0,), R + 2: (1, 2), LAST: (3,)}
+TENSOR_DEGREES = {R + 1: (0,), R + 2: (1, 2, 3)}
 FIRST = [range(4)] * 5 + [range(2)] + [range(4)] * 2
-GPSIMD_B0 = {R + 2: (0, 1), LAST: (2,)}
+GPSIMD_B0 = {R + 2: (0, 1), LAST: (2, 3)}
 LAST_PARTS = 2
-V03 = 0
 WARM = (4, 3)
 FINISH = {R + 2: (0,), LAST: (1, 2)}
 SCALAR_DEGREES = {R - 1: (0,), R + 1: (1,), R + 2: (2, 3)}
@@ -261,10 +260,6 @@ def tile_rgcn_layer_pa_kernel(tc, x, adj, wr, br, w0, b0, out):
                 sums[(b, m)] = spare[:, D * n : D * (n + 1)]
                 nc.gpsimd.tensor_tensor(out=sums[(b, m)], in0=raw[(b, m)], in1=bias_all[:, W0, :], op=ADD)
 
-        def add_b0_vector(m):
-            sums[(0, m)] = fin.tile([P, D], F32, tag="fsum", name="fsum", bufs=NT)
-            nc.vector.tensor_tensor(out=sums[(0, m)], in0=raw[(0, m)], in1=bias_all[:, W0, :], op=ADD)
-
         def add_b0_half(m, h):
             sums[(1, m, h)] = fin.tile([P, D // 2], F32, tag="hsum", name="hsum")
             nc.vector.tensor_tensor(out=sums[(1, m, h)], in0=acc[(1, m, h)], in1=bias_all[:, W0, half(h)], op=ADD)
@@ -326,7 +321,7 @@ def tile_rgcn_layer_pa_kernel(tc, x, adj, wr, br, w0, b0, out):
                     regroup_gpsimd(k + 1, 0, GPSIMD_GROUPS)
                     regroup(k + 1, nc.scalar.copy, GPSIMD_GROUPS, GROUPS)
 
-                for dc in range(NT if k < LAST else 2):
+                for dc in range(NT):
                     add_bias(k, dc)
 
                 def before(ms):
@@ -392,17 +387,6 @@ def tile_rgcn_layer_pa_kernel(tc, x, adj, wr, br, w0, b0, out):
                     for dc in range(NT):
                         messages(k + 1, dc)
 
-            quantise_part(mq[LAST], grouped[("m", LAST)], 0, 2)
-            for m in range(NT):
-                aggregate_half(LAST, m, 0)
-            if V03 == 0:
-                add_b0_vector(3)
-            add_bias(LAST, 2)
-            sum_den_vector(1)
-            add_bias(LAST, 3)
-            invert_den(1)
-            quantise_part(mq[LAST], grouped[("m", LAST)], 1, 2)
-
             def open_half(m):
                 for k in range(R, LAST):
                     aggregate_half(k, m, 1)
@@ -410,21 +394,15 @@ def tile_rgcn_layer_pa_kernel(tc, x, adj, wr, br, w0, b0, out):
 
             for m in range(2):
                 open_half(m)
-            if V03 == 1:
-                add_b0_vector(3)
-                finish(0, 3)
-            if V03 == 0:
-                finish(0, 3)
-            if V03 == 2:
-                add_b0_gpsimd(0, [3], LAST + 1)
-            for m in range(NT):
-                add_b0_half(m, 0)
-                finish(1, m, 0)
-            for m in range(NT):
-                if m >= 2:
-                    open_half(m)
-                aggregate_half(LAST, m, 1)
-                add_b0_half(m, 1)
-                finish(1, m, 1)
-                if V03 == 2 and m == 0:
-                    finish(0, 3)
+            sum_den_vector(1)
+            quantise_part(mq[LAST], grouped[("m", LAST)], 0, 2)
+            invert_den(1)
+            quantise_part(mq[LAST], grouped[("m", LAST)], 1, 2)
+            finish(0, 3)
+            for h in range(2):
+                for m in range(NT):
+                    if h == 1 and m >= 2:
+                        open_half(m)
+                    aggregate_half(LAST, m, h)
+                    add_b0_half(m, h)
+                    finish(1, m, h)

from contextlib import ExitStack

import concourse.mybir as mybir
from concourse.masks import make_identity

F32 = mybir.dt.float32
BF16 = mybir.dt.bfloat16
U32 = mybir.dt.uint32
U8 = mybir.dt.uint8
FP8X4 = mybir.dt.float8_e4m3fn_x4
ADD = mybir.AluOpType.add
MULT = mybir.AluOpType.mult
COPY = mybir.ActivationFunctionType.Copy
RELU = mybir.ActivationFunctionType.Relu
MAX = mybir.AluOpType.max

P = 128
B, R, N, D = 2, 4, 512, 512
NT = N // P
PACK = 4
W0 = R
ROUNDS = B * R
LAST = ROUNDS - 1
FLOPS = 2 * B * (R + 1) * N * D * D + 2 * B * N * R * N * D

ROWS = "(u p e) f -> p u e f"
TILES = "p (u e) f -> p u e f"

GROUPS = D // 4
GPSIMD_GROUPS = 80
TENSOR_RELATIONS = (2, 2)
TENSOR_DEGREES = {R + 1: (0,), R + 2: (1, 2, 3)}
FIRST = [range(4)] * 5 + [range(2)] + [range(4)] * 2
GPSIMD_B0 = {R + 2: (0, 1), LAST: (2, 3)}
LAST_PARTS = 2
WARM = (4, 3)
FINISH = {R + 2: (0,), LAST: (1, 2)}
SCALAR_DEGREES = {R - 1: (0,), R + 1: (1,), R + 2: (2, 3)}


def tile_rgcn_layer_pa_kernel(tc, x, adj, wr, br, w0, b0, out):
    nc = tc.nc
    with ExitStack() as ctx:
        const = ctx.enter_context(tc.tile_pool(name="const", bufs=1))
        inp = ctx.enter_context(tc.tile_pool(name="inp", bufs=1))
        keep = ctx.enter_context(tc.tile_pool(name="keep", bufs=1))
        grp = ctx.enter_context(tc.tile_pool(name="grp", bufs=B * R + B))
        ring = ctx.enter_context(tc.tile_pool(name="ring", bufs=1))
        fin = ctx.enter_context(tc.tile_pool(name="fin", bufs=B * NT))
        ps_acc = ctx.enter_context(tc.psum_pool(name="ps_acc", bufs=NT))
        ps_work = ctx.enter_context(tc.psum_pool(name="ps_work", bufs=4))

        ident_f = const.tile([P, P], F32, name="ident_f")
        ident_b = const.tile([P, P], BF16, name="ident_b")
        bias_rows = const.tile([P, D], BF16, name="brows")
        bias_all = const.tile([P, R + 1, D], BF16, name="bias_bc")
        ones = const.tile([P, 2], BF16, name="ones")
        warm = const.tile([P, D], BF16, name="warm")
        deg_tensor = const.tile([P, B * NT], F32, name="den_t")
        deg_scalar = const.tile([P, B * NT], F32, name="den_s")
        den = const.tile([P, B * NT], F32, name="den_one")
        inv_den = const.tile([P, B * NT], F32, name="rden")
        unread = const.tile([P, R * N], BF16, name="junk")

        x_sb = [inp.tile([P, NT, D], BF16, name="x_sb%d" % b) for b in range(B)]
        w_sb = [inp.tile([P, PACK, D], BF16, name="w_sb%d" % i) for i in range(R + 1)]
        adj_sb = [inp.tile([P, R, NT, N], BF16, name="adj_sb%d" % b) for b in range(B)]

        def load_x(b):
            nc.sync.dma_start(out=x_sb[b].rearrange(TILES, u=2), in_=x[b].rearrange(ROWS, u=2, e=2))

        def load_w(i):
            src = w0 if i == W0 else wr[i]
            nc.sync.dma_start(out=w_sb[i].rearrange(TILES, u=2), in_=src.rearrange(ROWS, u=2, e=2))

        def load_adj(b, r):
            nc.sync.dma_start(
                out=adj_sb[b][:, r].rearrange(TILES, u=2), in_=adj[b, r].rearrange(ROWS, u=2, e=2)
            )

        def packed(name):
            words = keep.tile([P, 512], U32, name=name + "_c", align_bytes=64)
            scales = keep.tile([P, 512], U8, name=name + "_s", align_bytes=64)
            return words, scales

        xq = [packed("xq%d" % b) for b in range(B)]
        wq = [packed("wq%d" % i) for i in range(R + 1)]
        aq = [packed("aq%d" % k) for k in range(ROUNDS)]
        mq = [packed("mq%d" % k) for k in range(ROUNDS)]

        def quantise(dst, src):
            nc.vector.quantize_mx(out=dst[0].bitcast(FP8X4), scales=dst[1], in_=src)

        def quantise_part(dst, src, part, parts):
            n = 512 // parts
            nc.vector.quantize_mx(
                out=dst[0][:, n * part : n * (part + 1)].bitcast(FP8X4),
                scales=dst[1][:, n * part : n * (part + 1)],
                in_=src[:, PACK * n * part : PACK * n * (part + 1)],
            )

        def mx_pass(acc, lhs, lcols, rhs, rcols, start, stop):
            nc.tensor.matmul_mx(
                out=acc,
                lhsT=lhs[0][:, lcols].bitcast(FP8X4),
                lhsT_scale=lhs[1][:, lcols],
                rhs=rhs[0][:, rcols].bitcast(FP8X4),
                rhs_scale=rhs[1][:, rcols],
                start=start,
                stop=stop,
            )

        def cols(i):
            return slice(P * i, P * (i + 1))

        def half(h):
            return slice(D // 2 * h, D // 2 * (h + 1))

        banks = {}
        grouped = {}

        def bias_spread(i):
            banks[("bias", i)] = ps_work.tile([P, D], BF16, tag="work", name="bias_ps")
            nc.tensor.matmul(
                out=banks[("bias", i)],
                lhsT=ident_b[:, i : i + 1].to_broadcast([P, P]),
                rhs=bias_rows,
                start=True,
                stop=True,
            )
            nc.scalar.copy(out=bias_all[:, i, :], in_=banks[("bias", i)])

        def flip(key, rows, h, pool, tag):
            if h == 0:
                grouped[key] = grp.tile([P, PACK * 512], BF16, tag="flipped", name="flipped", align_bytes=64)
            bank = pool.tile([P, 2, 2 * P], F32, tag=tag, name="flip_ps")
            for a in range(2):
                words_in = rows[:, 2 * h + a, :].bitcast(F32)
                for v in range(2):
                    nc.tensor.transpose(bank[:, v, cols(a)], words_in[:, cols(v)], ident_f)
            words_out = grouped[key].bitcast(F32).rearrange("q (c v) -> q c v", v=2)
            nc.scalar.copy(out=words_out[:, 2 * P * h : 2 * P * (h + 1), :], in_=bank.rearrange("q v c -> q c v"))

        def flip_adj(k, pool, tag):
            for h in range(2):
                flip(("a", k), adj_sb[k // R][:, k % R], h, pool, tag)

        def ring_tile(slot):
            return ring.tile([P, PACK * D], BF16, tag="ring%d" % (slot % 3), name="ring", align_bytes=64)

        def regroup_gpsimd(i, first, end):
            c0, c1 = 4 * first, 4 * end
            nc.gpsimd.tensor_scalar(
                out=grouped[("w", i)].rearrange("q (c t) -> q c t", t=PACK)[:, c0:c1],
                in0=w_sb[i].rearrange("q t c -> q c t")[:, c0:c1],
                scalar1=1.0,
                scalar2=0.0,
                op0=MULT,
                op1=ADD,
            )

        def regroup(i, copy, first, end):
            copy(
                out=grouped[("w", i)].rearrange("q (c i t) -> q c t i", i=4, t=PACK)[:, first:end],
                in_=w_sb[i].rearrange("q t (c i) -> q c t i", i=4)[:, first:end],
            )

        def warm_up(n):
            bank = ps_acc.tile([P, D], F32, tag="acc", name="warm_ps")
            for i in range(n):
                nc.tensor.matmul(out=bank, lhsT=warm[:, 0:P], rhs=warm, start=True, stop=True)

        def messages(k, dc):
            b, r = divmod(k, R)
            bank = ps_work.tile([P, NT, P], F32, tag="work", name="ms_ps")
            banks[("ms", k, dc)] = bank
            for t in range(NT):
                mx_pass(bank[:, t, :], xq[b], cols(t), wq[r], cols(dc), True, True)

        def add_bias(k, dc):
            nc.vector.tensor_tensor(
                out=grouped[("m", k)].rearrange("p (d t) -> p d t", t=PACK)[:, cols(dc), :],
                in0=banks[("ms", k, dc)].rearrange("p t d -> p d t"),
                in1=bias_all[:, k % R, cols(dc)].unsqueeze(2).to_broadcast([P, P, PACK]),
                op=ADD,
            )

        acc = {}

        def self_term(m):
            mx_pass(acc[(0, m)], xq[0], cols(m), wq[W0], slice(0, D), False, True)

        def aggregate(k, m):
            if k == 0:
                acc[(0, m)] = ps_acc.tile([P, D], F32, tag="acc", name="acc_ps")
            mx_pass(acc[(0, m)], aq[k], cols(m), mq[k], slice(0, D), k == 0, False)

        def self_half(m, h):
            mx_pass(acc[(1, m, h)], xq[1], cols(m), wq[W0], half(h), False, False)

        def aggregate_half(k, m, h):
            if k == R:
                pool, tag = (ps_acc, "acc") if h == 0 else (ps_work, "work")
                acc[(1, m, h)] = pool.tile([P, D // 2], F32, tag=tag, name="half_ps")
            mx_pass(acc[(1, m, h)], aq[k], cols(m), mq[k], half(h), k == R, k == LAST)

        def degrees_scalar(j):
            b, m = divmod(j, NT)
            nc.scalar.activation(
                out=unread.rearrange("p (r j) -> p r j", r=R)[:, TENSOR_RELATIONS[b] : R],
                in_=adj_sb[b][:, TENSOR_RELATIONS[b] : R, m, :],
                func=COPY,
                accum_out=deg_scalar[:, j : j + 1],
            )

        def degrees_tensor(j):
            b, m = divmod(j, NT)
            bank = ps_work.tile([P, 2], F32, tag="work", name="deg_ps")
            n = TENSOR_RELATIONS[b]
            for r in range(n):
                words = grouped[("a", R * b + r)].rearrange("q (c t) -> q c t", t=PACK)
                for t in range(PACK):
                    nc.tensor.matmul(
                        out=bank,
                        lhsT=words[:, cols(m), t],
                        rhs=ones,
                        start=(r == 0 and t == 0),
                        stop=(r == n - 1 and t == PACK - 1),
                    )
            nc.scalar.copy(out=deg_tensor[:, j : j + 1], in_=bank[:, 0:1])

        def sum_den(b):
            these = slice(NT * b, NT * (b + 1))
            nc.gpsimd.tensor_tensor(out=den[:, these], in0=deg_tensor[:, these], in1=deg_scalar[:, these], op=ADD)
            nc.gpsimd.tensor_scalar(
                out=den[:, these], in0=den[:, these], scalar1=1.0, scalar2=1.0, op0=MULT, op1=ADD
            )

        def sum_den_vector(b):
            these = slice(NT * b, NT * (b + 1))
            nc.vector.scalar_tensor_tensor(
                out=den[:, these], in0=deg_tensor[:, these], scalar=1.0, in1=deg_scalar[:, these], op0=ADD, op1=ADD
            )

        def invert_den(b):
            these = slice(NT * b, NT * (b + 1))
            nc.vector.reciprocal(out=inv_den[:, these], in_=den[:, these])

        sums = {}

        raw = {}

        def empty(b, m):
            raw[(b, m)] = fin.tile([P, D], F32, tag="raw", name="raw", bufs=NT)
            nc.scalar.copy(out=raw[(b, m)], in_=acc[(b, m)])

        def add_b0_gpsimd(b, ms, k):
            spare = ring_tile(k + 2).bitcast(F32)
            for n, m in enumerate(ms):
                sums[(b, m)] = spare[:, D * n : D * (n + 1)]
                nc.gpsimd.tensor_tensor(out=sums[(b, m)], in0=raw[(b, m)], in1=bias_all[:, W0, :], op=ADD)

        def add_b0_half(m, h):
            sums[(1, m, h)] = fin.tile([P, D // 2], F32, tag="hsum", name="hsum")
            nc.vector.tensor_tensor(out=sums[(1, m, h)], in0=acc[(1, m, h)], in1=bias_all[:, W0, half(h)], op=ADD)

        def finish(b, m, *h):
            n = half(*h) if h else slice(0, D)
            res = fin.tile([P, n.stop - n.start], F32, tag="hres" if h else "res", name="res", bufs=B * NT if h else NT)
            j = NT * b + m
            nc.scalar.activation(out=res, in_=sums[(b, m, *h)], func=RELU, scale=inv_den[:, j : j + 1])
            u, e = divmod(m, 2)
            nc.sync.dma_start(out=out[b].rearrange(ROWS, u=2, e=2)[:, u, e, n], in_=res)

        with tc.manual_schedule():
            nc.vector.memset(warm, 0.0)
            nc.vector.memset(bias_rows, 0.0)
            nc.vector.memset(ones, 1.0)
            make_identity(nc, ident_f)
            make_identity(nc, ident_b)
            for u in range(2):
                nc.sync.dma_start(
                    out=x_sb[0].rearrange(TILES, u=2)[:, u], in_=x[0].rearrange(ROWS, u=2, e=2)[:, u]
                )
            load_w(0)
            nc.sync.dma_start(out=bias_rows[0:R, :], in_=br)
            load_w(1)
            load_adj(0, 0)
            load_adj(0, 1)
            load_x(1)
            load_w(2)
            load_adj(0, 2)
            load_adj(0, 3)
            load_w(3)
            load_w(W0)
            for r in range(R):
                load_adj(1, r)
            nc.sync.dma_start(out=bias_all[:, W0, :], in_=b0.partition_broadcast(P))

            grouped[("w", 0)] = ring_tile(2)
            warm_up(WARM[0])
            for h in range(2):
                flip("x0", x_sb[0], h, ps_work, "work")
            warm_up(WARM[1])
            quantise_part(xq[0], grouped["x0"], 0, 2)
            regroup(0, nc.vector.tensor_copy, 0, GROUPS // 2)
            regroup(0, nc.scalar.copy, GROUPS // 2, GROUPS)
            quantise_part(xq[0], grouped["x0"], 1, 2)
            quantise_part(wq[0], grouped[("w", 0)], 0, 2)
            bias_spread(0)
            messages(0, 0)
            messages(0, 1)
            quantise_part(wq[0], grouped[("w", 0)], 1, 2)
            messages(0, 2)
            messages(0, 3)

            for k in range(ROUNDS):
                grouped[("m", k)] = ring_tile(k)
                if k < R:
                    grouped[("w", k + 1)] = ring_tile(k + 2)
                    regroup_gpsimd(k + 1, 0, GPSIMD_GROUPS)
                    regroup(k + 1, nc.scalar.copy, GPSIMD_GROUPS, GROUPS)

                for dc in range(NT):
                    add_bias(k, dc)

                def before(ms):
                    for m in ms:
                        if 1 <= k <= R:
                            aggregate(k - 1, m)
                        if k == R + 1:
                            self_term(m)
                            empty(0, m)
                        if k >= R + 2:
                            aggregate_half(k - 2, m, 0)

                before(FIRST[k])
                if 1 <= k <= R:
                    degrees_tensor(k - 1)

                if k == 0:
                    flip_adj(0, ps_acc, "acc")
                if k + 1 < R:
                    bias_spread(k + 1)
                if k == 0:
                    flip_adj(1, ps_acc, "acc")
                    for h in range(2):
                        flip("x1", x_sb[1], h, ps_acc, "acc")
                elif k < LAST:
                    flip_adj(k + 1, ps_work, "work")
                if k == R + 1:
                    for m in TENSOR_DEGREES.get(k, ()):
                        degrees_tensor(NT + m)
                before([m for m in range(NT) if m not in FIRST[k]])
                if k in GPSIMD_B0:
                    add_b0_gpsimd(0, GPSIMD_B0[k], k)
                if k == R + 1:
                    sum_den(0)
                if k != R + 1:
                    for m in TENSOR_DEGREES.get(k, ()):
                        degrees_tensor(NT + m)
                if 1 <= k <= R:
                    degrees_scalar(k - 1)
                for m in SCALAR_DEGREES.get(k, ()):
                    degrees_scalar(NT + m)
                if k == R + 1:
                    invert_den(0)
                if k == LAST:
                    for m in range(NT):
                        self_half(m, 0)
                        aggregate_half(k - 1, m, 0)
                for m in FINISH.get(k, ()):
                    finish(0, m)

                if k < R:
                    quantise(wq[k + 1], grouped[("w", k + 1)])
                if k < LAST:
                    quantise(aq[k], grouped[("a", k)])
                if k == 1:
                    quantise(xq[1], grouped["x1"])
                if k < LAST:
                    quantise(mq[k], grouped[("m", k)])
                if k == LAST - 1:
                    quantise(aq[LAST], grouped[("a", LAST)])

                if k < LAST:
                    for dc in range(NT):
                        messages(k + 1, dc)

            def open_half(m):
                for k in range(R, LAST):
                    aggregate_half(k, m, 1)
                self_half(m, 1)

            for m in range(2):
                open_half(m)
            sum_den_vector(1)
            quantise_part(mq[LAST], grouped[("m", LAST)], 0, 2)
            invert_den(1)
            quantise_part(mq[LAST], grouped[("m", LAST)], 1, 2)
            finish(0, 3)
            for h in range(2):
                for m in range(NT):
                    if h == 1 and m >= 2:
                        open_half(m)
                    aggregate_half(LAST, m, h)
                    add_b0_half(m, h)
                    finish(1, m, h)
